import numpy as np
import ml_dtypes

BF16 = ml_dtypes.bfloat16


def bf(x):
    return np.asarray(x, np.float32).astype(BF16)


def f32(x):
    return np.asarray(x, np.float32)


def f64(x):
    return np.asarray(x).astype(np.float64)


def striped(idx):
    return np.tile(idx.reshape(-1, 16).T, (8, 1))


S, D, E, A, F, T, N, H, K = 256, 128, 128, 128, 256, 4, 1024, 128, 8
EPS = 1e-5


def sigmoid(v):
    return 1.0 / (1.0 + np.exp(-v))


def softplus(v):
    return np.log(1.0 + np.exp(v))


def setup_inputs():
    sc = 1.0 / np.sqrt(D + D + E)
    idx = np.concatenate([np.random.permutation(S)[:H] for _ in range(K)])
    return {"table": bf(np.random.standard_normal((S, D))), "w_self": bf(sc * np.random.standard_normal((D, F))), "w_nbr": bf(sc * np.random.standard_normal((D, F))), "w_edge": bf(sc * np.random.standard_normal((E, F))), "edge": bf(np.random.standard_normal((E, N))), "gamma1": f32(1.0 + 0.1 * np.random.standard_normal((F, 1))), "beta1": f32(0.1 * np.random.standard_normal((F, 1))), "offs": striped(idx)}


def reference(table, w_self, w_nbr, w_edge, edge, gamma1, beta1, offs):
    idx = offs[:16].T.reshape(-1)
    tab = f64(table)
    z = f64(w_nbr).T @ tab[idx].T + np.repeat(f64(w_self).T @ tab.T, T, axis=1) + f64(w_edge).T @ f64(edge)
    mean = z.mean(axis=1, keepdims=True)
    var = ((z - mean) ** 2).mean(axis=1, keepdims=True)
    y = (z - mean) / np.sqrt(var + EPS) * f64(gamma1) + f64(beta1)
    prod = sigmoid(y[:A]) * softplus(y[A:])
    return prod.reshape(A, S, T).sum(axis=2)

@@ -1,0 +1,133 @@
+import concourse.mybir as mybir
+from concourse.masks import make_identity
+
+P = 128
+S, D, E, F, T, N = 256, 128, 128, 256, 4, 1024
+EPS = 1e-5
+PIECE = S
+NPIECE = N // PIECE
+ATOMS = PIECE // T
+GATE, CORE = 0, 1
+CLAMP = 30.0
+FLOPS = 2 * F * (N * D + S * D + N * E)
+
+BF16, F32, U16 = mybir.dt.bfloat16, mybir.dt.float32, mybir.dt.uint16
+ALU = mybir.AluOpType
+FUNC = mybir.ActivationFunctionType
+
+
+def tile_convlayer_kernel(tc, table, w_self, w_nbr, w_edge, edge, gamma1, beta1, offs, out):
+    nc = tc.nc
+    with (
+        tc.tile_pool(name="held", bufs=1) as held,
+        tc.psum_pool(name="banks", bufs=8) as banks,
+    ):
+        offsets = held.tile([P, N // 16], U16, name="offsets")
+        nc.sync.dma_start(offsets[:], offs)
+        rows = held.tile([P, S // P, D], BF16, name="rows")
+        nc.sync.dma_start(rows[:], table.rearrange("(b p) d -> p b d", p=P))
+        w_edge_sb = held.tile([P, F], BF16, name="w_edge_sb")
+        nc.scalar.dma_start(w_edge_sb[:], w_edge)
+        edge_sb = held.tile([P, N], BF16, name="edge_sb")
+        nc.scalar.dma_start(edge_sb[:], edge)
+        w_self_sb = held.tile([P, F], BF16, name="w_self_sb")
+        nc.sync.dma_start(w_self_sb[:], w_self)
+        w_nbr_sb = held.tile([P, F], BF16, name="w_nbr_sb")
+        nc.sync.dma_start(w_nbr_sb[:], w_nbr)
+        gamma_sb = held.tile([P, 2], F32, name="gamma_sb")
+        beta_sb = held.tile([P, 2], F32, name="beta_sb")
+        with nc.allow_non_contiguous_dma(reason="one float to a partition, 256 in all"):
+            nc.gpsimd.dma_start(gamma_sb[:], gamma1.rearrange("(b p) o -> p (b o)", p=P))
+            nc.gpsimd.dma_start(beta_sb[:], beta1.rearrange("(b p) o -> p (b o)", p=P))
+
+        ident = held.tile([P, P], BF16, name="ident")
+        make_identity(nc, ident[:])
+        neg_half = held.tile([P, 1], F32, name="neg_half")
+        nc.gpsimd.memset(neg_half[:], -0.5)
+        one = held.tile([P, 1], F32, name="one")
+        nc.gpsimd.memset(one[:], 1.0)
+
+        half_gamma = held.tile([P, 2], F32, name="half_gamma")
+        nc.vector.tensor_scalar_mul(half_gamma[:], gamma_sb[:], 0.5)
+        half_beta = held.tile([P, 2], F32, name="half_beta")
+        nc.vector.tensor_scalar_mul(half_beta[:], beta_sb[:], 0.5)
+
+        flipped = banks.tile([P, S], BF16, tag="bank", name="flipped")
+        for b in range(S // P):
+            nc.tensor.transpose(flipped[:, b * P : (b + 1) * P], rows[:, b, :], ident[:])
+        tab_t = held.tile([P, S], BF16, name="tab_t")
+        nc.vector.tensor_copy(tab_t[:], flipped[:])
+
+        z = [[banks.tile([P, PIECE], F32, tag="bank", name=f"z{blk}_{k}") for k in range(NPIECE)] for blk in range(2)]
+        groups = [(blk, k) for blk in (GATE, CORE) for k in range(NPIECE)]
+        for blk, k in groups:
+            nc.tensor.matmul(
+                z[blk][k][:],
+                w_edge_sb[:, blk * P : (blk + 1) * P],
+                edge_sb[:, k * PIECE : (k + 1) * PIECE],
+                start=True,
+                stop=False,
+            )
+        for blk, k in groups:
+            own = tab_t[:, k * ATOMS : (k + 1) * ATOMS].unsqueeze(2).to_broadcast([P, ATOMS, T])
+            nc.tensor.matmul(
+                z[blk][k][:].rearrange("p (i t) -> p i t", t=T),
+                w_self_sb[:, blk * P : (blk + 1) * P],
+                own,
+                start=False,
+                stop=False,
+            )
+        for blk, k in groups:
+            neighbours = tab_t[:].indirect(offsets[:, k * (PIECE // 16) : (k + 1) * (PIECE // 16)])
+            nc.tensor.matmul(z[blk][k][:], w_nbr_sb[:, blk * P : (blk + 1) * P], neighbours, start=False, stop=True)
+
+        stats = held.tile([P, 2, NPIECE, 6], F32, name="stats")
+        moments = held.tile([P, 2, 2], F32, name="moments")
+        var_eps = held.tile([P, 2], F32, name="var_eps")
+        rstd = held.tile([P, 2], F32, name="rstd")
+        scale = held.tile([P, 2], F32, name="scale")
+        mean_scaled = held.tile([P, 2], F32, name="mean_scaled")
+        shift = held.tile([P, 2], F32, name="shift")
+        for blk in (GATE, CORE):
+            col = slice(blk, blk + 1)
+            for k in range(NPIECE):
+                nc.vector.bn_stats(stats[:, blk, k, :], z[blk][k][:])
+            nc.vector.bn_aggr(moments[:, blk, :], stats[:, blk, :, :])
+            nc.vector.tensor_scalar_add(var_eps[:, col], moments[:, blk, 1:2], EPS)
+            nc.gpsimd.tensor_tensor(rstd[:, col], var_eps[:, col], neg_half[:], ALU.pow)
+            nc.vector.tensor_mul(scale[:, col], half_gamma[:, col], rstd[:, col])
+            nc.vector.tensor_mul(mean_scaled[:, col], moments[:, blk, 0:1], scale[:, col])
+            nc.vector.tensor_sub(shift[:, col], half_beta[:, col], mean_scaled[:, col])
+
+        tanh_g = held.tile([P, N], F32, name="tanh_g")
+        half_y = held.tile([P, N], F32, name="half_y")
+        clamped = held.tile([P, N], F32, name="clamped")
+        expo = held.tile([P, N], F32, name="expo")
+        log1p = held.tile([P, N], F32, name="log1p")
+        half_sp = held.tile([P, N], F32, name="half_sp")
+        prod = held.tile([P, N], F32, name="prod")
+        out_sb = held.tile([P, S], F32, name="out_sb")
+        for k in range(NPIECE):
+            cols = slice(k * PIECE, (k + 1) * PIECE)
+            nc.scalar.activation(
+                tanh_g[:, cols], z[GATE][k][:], FUNC.Tanh, bias=shift[:, GATE : GATE + 1], scale=scale[:, GATE : GATE + 1]
+            )
+        for k in range(NPIECE):
+            cols = slice(k * PIECE, (k + 1) * PIECE)
+            nc.vector.tensor_scalar(
+                half_y[:, cols], z[CORE][k][:], scale[:, CORE : CORE + 1], shift[:, CORE : CORE + 1], ALU.mult, ALU.add
+            )
+            nc.vector.tensor_scalar_min(clamped[:, cols], half_y[:, cols], CLAMP / 2)
+            nc.scalar.activation(expo[:, cols], clamped[:, cols], FUNC.Exp, scale=2.0)
+        for k in range(NPIECE):
+            cols = slice(k * PIECE, (k + 1) * PIECE)
+            nc.scalar.activation(log1p[:, cols], expo[:, cols], FUNC.Ln, bias=one[:])
+            nc.vector.scalar_tensor_tensor(half_sp[:, cols], log1p[:, cols], 0.5, half_y[:, cols], ALU.mult, ALU.max)
+            nc.vector.scalar_tensor_tensor(prod[:, cols], tanh_g[:, cols], 1.0, half_sp[:, cols], ALU.add, ALU.mult)
+            nc.vector.tensor_reduce(
+                out_sb[:, k * ATOMS : (k + 1) * ATOMS],
+                prod[:, cols].rearrange("p (i t) -> p i t", t=T),
+                axis=mybir.AxisListType.X,
+                op=ALU.add,
+            )
+        nc.sync.dma_start(out, out_sb[:])

@@ -22,8 +22,13 @@ def tile_convlayer_kernel(tc, table, w_self, w_nbr, w_edge, edge, gamma1, beta1,
         tc.tile_pool(name="held", bufs=1) as held,
         tc.psum_pool(name="banks", bufs=8) as banks,
     ):
-        offsets = held.tile([P, N // 16], U16, name="offsets")
-        nc.sync.dma_start(offsets[:], offs)
+        ident = held.tile([P, P], BF16, name="ident")
+        make_identity(nc, ident[:])
+        neg_half = held.tile([P, 1], F32, name="neg_half")
+        nc.gpsimd.memset(neg_half[:], -0.5)
+        one = held.tile([P, 1], F32, name="one")
+        nc.gpsimd.memset(one[:], 1.0)
+
         rows = held.tile([P, S // P, D], BF16, name="rows")
         nc.sync.dma_start(rows[:], table.rearrange("(b p) d -> p b d", p=P))
         w_edge_sb = held.tile([P, F], BF16, name="w_edge_sb")
@@ -32,25 +37,24 @@ def tile_convlayer_kernel(tc, table, w_self, w_nbr, w_edge, edge, gamma1, beta1,
         nc.scalar.dma_start(edge_sb[:], edge)
         w_self_sb = held.tile([P, F], BF16, name="w_self_sb")
         nc.sync.dma_start(w_self_sb[:], w_self)
+        offsets = held.tile([P, N // 16], U16, name="offsets")
+        nc.sync.dma_start(offsets[:], offs)
         w_nbr_sb = held.tile([P, F], BF16, name="w_nbr_sb")
         nc.sync.dma_start(w_nbr_sb[:], w_nbr)
         gamma_sb = held.tile([P, 2], F32, name="gamma_sb")
         beta_sb = held.tile([P, 2], F32, name="beta_sb")
         with nc.allow_non_contiguous_dma(reason="one float to a partition, 256 in all"):
-            nc.gpsimd.dma_start(gamma_sb[:], gamma1.rearrange("(b p) o -> p (b o)", p=P))
-            nc.gpsimd.dma_start(beta_sb[:], beta1.rearrange("(b p) o -> p (b o)", p=P))
-
-        ident = held.tile([P, P], BF16, name="ident")
-        make_identity(nc, ident[:])
-        neg_half = held.tile([P, 1], F32, name="neg_half")
-        nc.gpsimd.memset(neg_half[:], -0.5)
-        one = held.tile([P, 1], F32, name="one")
-        nc.gpsimd.memset(one[:], 1.0)
+            nc.sync.dma_start(gamma_sb[:], gamma1.rearrange("(b p) o -> p (b o)", p=P))
+            nc.sync.dma_start(beta_sb[:], beta1.rearrange("(b p) o -> p (b o)", p=P))
 
         half_gamma = held.tile([P, 2], F32, name="half_gamma")
         nc.vector.tensor_scalar_mul(half_gamma[:], gamma_sb[:], 0.5)
+        neg_half_gamma = held.tile([P, 2], F32, name="neg_half_gamma")
+        nc.vector.tensor_scalar_mul(neg_half_gamma[:], gamma_sb[:], -0.5)
         half_beta = held.tile([P, 2], F32, name="half_beta")
         nc.vector.tensor_scalar_mul(half_beta[:], beta_sb[:], 0.5)
+        ceiling = held.tile([P, 1], F32, name="ceiling")
+        nc.vector.tensor_scalar(ceiling[:], beta_sb[:, CORE : CORE + 1], -0.5, CLAMP / 2, ALU.mult, ALU.add)
 
         flipped = banks.tile([P, S], BF16, tag="bank", name="flipped")
         for b in range(S // P):
@@ -58,11 +62,13 @@ def tile_convlayer_kernel(tc, table, w_self, w_nbr, w_edge, edge, gamma1, beta1,
         tab_t = held.tile([P, S], BF16, name="tab_t")
         nc.vector.tensor_copy(tab_t[:], flipped[:])
 
-        z = [[banks.tile([P, PIECE], F32, tag="bank", name=f"z{blk}_{k}") for k in range(NPIECE)] for blk in range(2)]
-        groups = [(blk, k) for blk in (GATE, CORE) for k in range(NPIECE)]
+        groups = [(blk, k) for blk in (CORE, GATE) for k in range(NPIECE)]
+        z = {}
+        for blk, k in groups:
+            z[blk, k] = banks.tile([P, PIECE], F32, tag="bank", name=f"z{blk}_{k}")
         for blk, k in groups:
             nc.tensor.matmul(
-                z[blk][k][:],
+                z[blk, k][:],
                 w_edge_sb[:, blk * P : (blk + 1) * P],
                 edge_sb[:, k * PIECE : (k + 1) * PIECE],
                 start=True,
@@ -71,7 +77,7 @@ def tile_convlayer_kernel(tc, table, w_self, w_nbr, w_edge, edge, gamma1, beta1,
         for blk, k in groups:
             own = tab_t[:, k * ATOMS : (k + 1) * ATOMS].unsqueeze(2).to_broadcast([P, ATOMS, T])
             nc.tensor.matmul(
-                z[blk][k][:].rearrange("p (i t) -> p i t", t=T),
+                z[blk, k][:].rearrange("p (i t) -> p i t", t=T),
                 w_self_sb[:, blk * P : (blk + 1) * P],
                 own,
                 start=False,
@@ -79,55 +85,70 @@ def tile_convlayer_kernel(tc, table, w_self, w_nbr, w_edge, edge, gamma1, beta1,
             )
         for blk, k in groups:
             neighbours = tab_t[:].indirect(offsets[:, k * (PIECE // 16) : (k + 1) * (PIECE // 16)])
-            nc.tensor.matmul(z[blk][k][:], w_nbr_sb[:, blk * P : (blk + 1) * P], neighbours, start=False, stop=True)
+            nc.tensor.matmul(z[blk, k][:], w_nbr_sb[:, blk * P : (blk + 1) * P], neighbours, start=False, stop=True)
 
         stats = held.tile([P, 2, NPIECE, 6], F32, name="stats")
         moments = held.tile([P, 2, 2], F32, name="moments")
         var_eps = held.tile([P, 2], F32, name="var_eps")
         rstd = held.tile([P, 2], F32, name="rstd")
-        scale = held.tile([P, 2], F32, name="scale")
-        mean_scaled = held.tile([P, 2], F32, name="mean_scaled")
-        shift = held.tile([P, 2], F32, name="shift")
-        for blk in (GATE, CORE):
-            col = slice(blk, blk + 1)
+        for blk in (CORE, GATE):
             for k in range(NPIECE):
-                nc.vector.bn_stats(stats[:, blk, k, :], z[blk][k][:])
+                nc.vector.bn_stats(stats[:, blk, k, :], z[blk, k][:])
             nc.vector.bn_aggr(moments[:, blk, :], stats[:, blk, :, :])
-            nc.vector.tensor_scalar_add(var_eps[:, col], moments[:, blk, 1:2], EPS)
-            nc.gpsimd.tensor_tensor(rstd[:, col], var_eps[:, col], neg_half[:], ALU.pow)
-            nc.vector.tensor_mul(scale[:, col], half_gamma[:, col], rstd[:, col])
-            nc.vector.tensor_mul(mean_scaled[:, col], moments[:, blk, 0:1], scale[:, col])
-            nc.vector.tensor_sub(shift[:, col], half_beta[:, col], mean_scaled[:, col])
+            nc.vector.tensor_scalar_add(var_eps[:, blk : blk + 1], moments[:, blk, 1:2], EPS)
+            nc.gpsimd.tensor_tensor(rstd[:, blk : blk + 1], var_eps[:, blk : blk + 1], neg_half[:], ALU.pow)
+        pieces = [slice(k * PIECE, (k + 1) * PIECE) for k in range(NPIECE)]
 
-        tanh_g = held.tile([P, N], F32, name="tanh_g")
-        half_y = held.tile([P, N], F32, name="half_y")
+        neg_mean = held.tile([P, 1], F32, name="neg_mean")
+        nc.vector.tensor_scalar_mul(neg_mean[:], moments[:, CORE, 0:1], -1.0)
+        centred = held.tile([P, N], F32, name="centred")
+        for k in range(NPIECE):
+            nc.scalar.activation(centred[:, pieces[k]], z[CORE, k][:], FUNC.Identity, bias=neg_mean[:])
+        scale_c = held.tile([P, 1], F32, name="scale_c")
+        nc.vector.tensor_mul(scale_c[:], half_gamma[:, CORE : CORE + 1], rstd[:, CORE : CORE + 1])
         clamped = held.tile([P, N], F32, name="clamped")
         expo = held.tile([P, N], F32, name="expo")
+        for k in range(NPIECE):
+            nc.vector.tensor_scalar(clamped[:, pieces[k]], centred[:, pieces[k]], scale_c[:], ceiling[:], ALU.mult, ALU.min)
+            nc.scalar.activation(
+                expo[:, pieces[k]], clamped[:, pieces[k]], FUNC.Exp, bias=beta_sb[:, CORE : CORE + 1], scale=2.0
+            )
+        half_y = held.tile([P, N], F32, name="half_y")
+        for k in range(NPIECE):
+            nc.vector.tensor_scalar(
+                half_y[:, pieces[k]], centred[:, pieces[k]], scale_c[:], half_beta[:, CORE : CORE + 1], ALU.mult, ALU.add
+            )
+
+        neg_mean_gamma = held.tile([P, 1], F32, name="neg_mean_gamma")
+        nc.vector.tensor_mul(neg_mean_gamma[:], moments[:, GATE, 0:1], neg_half_gamma[:, GATE : GATE + 1])
+        scale_g = held.tile([P, 1], F32, name="scale_g")
+        nc.vector.tensor_mul(scale_g[:], half_gamma[:, GATE : GATE + 1], rstd[:, GATE : GATE + 1])
+        shift_g = held.tile([P, 1], F32, name="shift_g")
+        nc.vector.tensor_scalar(
+            shift_g[:], neg_mean_gamma[:], rstd[:, GATE : GATE + 1], half_beta[:, GATE : GATE + 1], ALU.mult, ALU.add
+        )
+        tanh_g = held.tile([P, N], F32, name="tanh_g")
+        for k in range(NPIECE):
+            nc.scalar.activation(tanh_g[:, pieces[k]], z[GATE, k][:], FUNC.Tanh, bias=shift_g[:], scale=scale_g[:])
+
         log1p = held.tile([P, N], F32, name="log1p")
         half_sp = held.tile([P, N], F32, name="half_sp")
         prod = held.tile([P, N], F32, name="prod")
         out_sb = held.tile([P, S], F32, name="out_sb")
         for k in range(NPIECE):
-            cols = slice(k * PIECE, (k + 1) * PIECE)
-            nc.scalar.activation(
-                tanh_g[:, cols], z[GATE][k][:], FUNC.Tanh, bias=shift[:, GATE : GATE + 1], scale=scale[:, GATE : GATE + 1]
+            nc.scalar.activation(log1p[:, pieces[k]], expo[:, pieces[k]], FUNC.Ln, bias=one[:])
+            nc.vector.scalar_tensor_tensor(
+                half_sp[:, pieces[k]], log1p[:, pieces[k]], 0.5, half_y[:, pieces[k]], ALU.mult, ALU.max
             )
-        for k in range(NPIECE):
-            cols = slice(k * PIECE, (k + 1) * PIECE)
-            nc.vector.tensor_scalar(
-                half_y[:, cols], z[CORE][k][:], scale[:, CORE : CORE + 1], shift[:, CORE : CORE + 1], ALU.mult, ALU.add
+            nc.vector.scalar_tensor_tensor(
+                prod[:, pieces[k]], tanh_g[:, pieces[k]], 1.0, half_sp[:, pieces[k]], ALU.add, ALU.mult
             )
-            nc.vector.tensor_scalar_min(clamped[:, cols], half_y[:, cols], CLAMP / 2)
-            nc.scalar.activation(expo[:, cols], clamped[:, cols], FUNC.Exp, scale=2.0)
-        for k in range(NPIECE):
-            cols = slice(k * PIECE, (k + 1) * PIECE)
-            nc.scalar.activation(log1p[:, cols], expo[:, cols], FUNC.Ln, bias=one[:])
-            nc.vector.scalar_tensor_tensor(half_sp[:, cols], log1p[:, cols], 0.5, half_y[:, cols], ALU.mult, ALU.max)
-            nc.vector.scalar_tensor_tensor(prod[:, cols], tanh_g[:, cols], 1.0, half_sp[:, cols], ALU.add, ALU.mult)
             nc.vector.tensor_reduce(
                 out_sb[:, k * ATOMS : (k + 1) * ATOMS],
-                prod[:, cols].rearrange("p (i t) -> p i t", t=T),
+                prod[:, pieces[k]].rearrange("p (i t) -> p i t", t=T),
                 axis=mybir.AxisListType.X,
                 op=ALU.add,
             )
-        nc.sync.dma_start(out, out_sb[:])
+            if k % 2 == 1:
+                half = slice((k - 1) * ATOMS, (k + 1) * ATOMS)
+                nc.sync.dma_start(out[:, half], out_sb[:, half])

@@ -9,6 +9,7 @@ NPIECE = N // PIECE
 ATOMS = PIECE // T
 GATE, CORE = 0, 1
 CLAMP = 30.0
+WARM_UP = 6
 FLOPS = 2 * F * (N * D + S * D + N * E)
 
 BF16, F32, U16 = mybir.dt.bfloat16, mybir.dt.float32, mybir.dt.uint16
@@ -28,6 +29,12 @@ def tile_convlayer_kernel(tc, table, w_self, w_nbr, w_edge, edge, gamma1, beta1,
         nc.gpsimd.memset(neg_half[:], -0.5)
         one = held.tile([P, 1], F32, name="one")
         nc.gpsimd.memset(one[:], 1.0)
+
+        zeros = held.tile([P, 512], BF16, name="zeros")
+        nc.vector.memset(zeros[:], 0.0)
+        unread = banks.tile([P, 512], F32, tag="bank", name="unread")
+        for turn in range(WARM_UP):
+            nc.tensor.matmul(unread[:], zeros[:, 0:P], zeros[:], start=True, stop=True)
 
         rows = held.tile([P, S // P, D], BF16, name="rows")
         nc.sync.dma_start(rows[:], table.rearrange("(b p) d -> p b d", p=P))

@@ -9,7 +9,6 @@ NPIECE = N // PIECE
 ATOMS = PIECE // T
 GATE, CORE = 0, 1
 CLAMP = 30.0
-WARM_UP = 6
 FLOPS = 2 * F * (N * D + S * D + N * E)
 
 BF16, F32, U16 = mybir.dt.bfloat16, mybir.dt.float32, mybir.dt.uint16
@@ -19,6 +18,9 @@ FUNC = mybir.ActivationFunctionType
 
 def tile_convlayer_kernel(tc, table, w_self, w_nbr, w_edge, edge, gamma1, beta1, offs, out):
     nc = tc.nc
+    pieces = [slice(k * PIECE, (k + 1) * PIECE) for k in range(NPIECE)]
+    atoms = [slice(k * ATOMS, (k + 1) * ATOMS) for k in range(NPIECE)]
+    features = [slice(blk * P, (blk + 1) * P) for blk in range(2)]
     with (
         tc.tile_pool(name="held", bufs=1) as held,
         tc.psum_pool(name="banks", bufs=8) as banks,
@@ -30,18 +32,13 @@ def tile_convlayer_kernel(tc, table, w_self, w_nbr, w_edge, edge, gamma1, beta1,
         one = held.tile([P, 1], F32, name="one")
         nc.gpsimd.memset(one[:], 1.0)
 
-        zeros = held.tile([P, 512], BF16, name="zeros")
-        nc.vector.memset(zeros[:], 0.0)
-        unread = banks.tile([P, 512], F32, tag="bank", name="unread")
-        for turn in range(WARM_UP):
-            nc.tensor.matmul(unread[:], zeros[:, 0:P], zeros[:], start=True, stop=True)
-
         rows = held.tile([P, S // P, D], BF16, name="rows")
         nc.sync.dma_start(rows[:], table.rearrange("(b p) d -> p b d", p=P))
         w_edge_sb = held.tile([P, F], BF16, name="w_edge_sb")
         nc.scalar.dma_start(w_edge_sb[:], w_edge)
         edge_sb = held.tile([P, N], BF16, name="edge_sb")
-        nc.scalar.dma_start(edge_sb[:], edge)
+        for k in range(NPIECE):
+            nc.scalar.dma_start(edge_sb[:, pieces[k]], edge[:, pieces[k]])
         w_self_sb = held.tile([P, F], BF16, name="w_self_sb")
         nc.sync.dma_start(w_self_sb[:], w_self)
         offsets = held.tile([P, N // 16], U16, name="offsets")
@@ -53,15 +50,15 @@ def tile_convlayer_kernel(tc, table, w_self, w_nbr, w_edge, edge, gamma1, beta1,
         with nc.allow_non_contiguous_dma(reason="one float to a partition, 256 in all"):
             nc.sync.dma_start(gamma_sb[:], gamma1.rearrange("(b p) o -> p (b o)", p=P))
             nc.sync.dma_start(beta_sb[:], beta1.rearrange("(b p) o -> p (b o)", p=P))
+        gamma_c, beta_c = gamma_sb[:, CORE : CORE + 1], beta_sb[:, CORE : CORE + 1]
 
-        half_gamma = held.tile([P, 2], F32, name="half_gamma")
-        nc.vector.tensor_scalar_mul(half_gamma[:], gamma_sb[:], 0.5)
-        neg_half_gamma = held.tile([P, 2], F32, name="neg_half_gamma")
-        nc.vector.tensor_scalar_mul(neg_half_gamma[:], gamma_sb[:], -0.5)
-        half_beta = held.tile([P, 2], F32, name="half_beta")
-        nc.vector.tensor_scalar_mul(half_beta[:], beta_sb[:], 0.5)
         ceiling = held.tile([P, 1], F32, name="ceiling")
-        nc.vector.tensor_scalar(ceiling[:], beta_sb[:, CORE : CORE + 1], -0.5, CLAMP / 2, ALU.mult, ALU.add)
+        nc.vector.tensor_scalar(ceiling[:], beta_c, -1.0, CLAMP, ALU.mult, ALU.add)
+        factors = held.tile([P, 2], F32, name="factors")
+        nc.vector.tensor_copy(factors[:, 0:1], gamma_sb[:, GATE : GATE + 1])
+        addends = held.tile([P, 2], F32, name="addends")
+        nc.vector.memset(addends[:, 0:1], 0.0)
+        nc.vector.tensor_copy(addends[:, 1:2], beta_sb[:, GATE : GATE + 1])
 
         flipped = banks.tile([P, S], BF16, tag="bank", name="flipped")
         for b in range(S // P):
@@ -69,89 +66,86 @@ def tile_convlayer_kernel(tc, table, w_self, w_nbr, w_edge, edge, gamma1, beta1,
         tab_t = held.tile([P, S], BF16, name="tab_t")
         nc.vector.tensor_copy(tab_t[:], flipped[:])
 
-        groups = [(blk, k) for blk in (CORE, GATE) for k in range(NPIECE)]
         z = {}
-        for blk, k in groups:
-            z[blk, k] = banks.tile([P, PIECE], F32, tag="bank", name=f"z{blk}_{k}")
-        for blk, k in groups:
+        for blk in (CORE, GATE):
+            for k in range(NPIECE):
+                z[blk, k] = banks.tile([P, PIECE], F32, tag="bank", name=f"z{blk}_{k}")
+
+        def edge_product(blk, k, start, stop):
+            nc.tensor.matmul(z[blk, k][:], w_edge_sb[:, features[blk]], edge_sb[:, pieces[k]], start=start, stop=stop)
+
+        def own_product(blk, k, start, stop):
+            own = tab_t[:, atoms[k]].unsqueeze(2).to_broadcast([P, ATOMS, T])
             nc.tensor.matmul(
-                z[blk, k][:],
-                w_edge_sb[:, blk * P : (blk + 1) * P],
-                edge_sb[:, k * PIECE : (k + 1) * PIECE],
-                start=True,
-                stop=False,
+                z[blk, k][:].rearrange("p (i t) -> p i t", t=T), w_self_sb[:, features[blk]], own, start=start, stop=stop
             )
-        for blk, k in groups:
-            own = tab_t[:, k * ATOMS : (k + 1) * ATOMS].unsqueeze(2).to_broadcast([P, ATOMS, T])
-            nc.tensor.matmul(
-                z[blk, k][:].rearrange("p (i t) -> p i t", t=T),
-                w_self_sb[:, blk * P : (blk + 1) * P],
-                own,
-                start=False,
-                stop=False,
-            )
-        for blk, k in groups:
+
+        def neighbour_product(blk, k, start, stop):
             neighbours = tab_t[:].indirect(offsets[:, k * (PIECE // 16) : (k + 1) * (PIECE // 16)])
-            nc.tensor.matmul(z[blk, k][:], w_nbr_sb[:, blk * P : (blk + 1) * P], neighbours, start=False, stop=True)
+            nc.tensor.matmul(z[blk, k][:], w_nbr_sb[:, features[blk]], neighbours, start=start, stop=stop)
+
+        for k in range(NPIECE):
+            edge_product(CORE, k, start=True, stop=False)
+        for k in range(NPIECE):
+            own_product(CORE, k, start=False, stop=False)
+        for k in range(NPIECE):
+            neighbour_product(CORE, k, start=False, stop=True)
+        for k in range(NPIECE):
+            neighbour_product(GATE, k, start=True, stop=False)
+        for k in range(NPIECE):
+            edge_product(GATE, k, start=False, stop=False)
+            own_product(GATE, k, start=False, stop=True)
 
         stats = held.tile([P, 2, NPIECE, 6], F32, name="stats")
         moments = held.tile([P, 2, 2], F32, name="moments")
-        var_eps = held.tile([P, 2], F32, name="var_eps")
         rstd = held.tile([P, 2], F32, name="rstd")
-        for blk in (CORE, GATE):
+
+        def normalise(blk):
             for k in range(NPIECE):
                 nc.vector.bn_stats(stats[:, blk, k, :], z[blk, k][:])
+                if k == 0:
+                    nc.vector.tensor_scalar_add(stats[:, blk, 0, 2:3], stats[:, blk, 0, 2:3], N * EPS)
             nc.vector.bn_aggr(moments[:, blk, :], stats[:, blk, :, :])
-            nc.vector.tensor_scalar_add(var_eps[:, blk : blk + 1], moments[:, blk, 1:2], EPS)
-            nc.gpsimd.tensor_tensor(rstd[:, blk : blk + 1], var_eps[:, blk : blk + 1], neg_half[:], ALU.pow)
-        pieces = [slice(k * PIECE, (k + 1) * PIECE) for k in range(NPIECE)]
+            nc.gpsimd.tensor_tensor(rstd[:, blk : blk + 1], moments[:, blk, 1:2], neg_half[:], ALU.pow)
 
-        neg_mean = held.tile([P, 1], F32, name="neg_mean")
-        nc.vector.tensor_scalar_mul(neg_mean[:], moments[:, CORE, 0:1], -1.0)
+        normalise(CORE)
+        neg_mean_gamma = held.tile([P, 1], F32, name="neg_mean_gamma")
+        nc.vector.scalar_tensor_tensor(neg_mean_gamma[:], moments[:, CORE, 0:1], -1.0, gamma_c, ALU.mult, ALU.mult)
         centred = held.tile([P, N], F32, name="centred")
         for k in range(NPIECE):
-            nc.scalar.activation(centred[:, pieces[k]], z[CORE, k][:], FUNC.Identity, bias=neg_mean[:])
-        scale_c = held.tile([P, 1], F32, name="scale_c")
-        nc.vector.tensor_mul(scale_c[:], half_gamma[:, CORE : CORE + 1], rstd[:, CORE : CORE + 1])
+            nc.scalar.activation(centred[:, pieces[k]], z[CORE, k][:], FUNC.Identity, bias=neg_mean_gamma[:], scale=gamma_c)
         clamped = held.tile([P, N], F32, name="clamped")
         expo = held.tile([P, N], F32, name="expo")
         for k in range(NPIECE):
-            nc.vector.tensor_scalar(clamped[:, pieces[k]], centred[:, pieces[k]], scale_c[:], ceiling[:], ALU.mult, ALU.min)
-            nc.scalar.activation(
-                expo[:, pieces[k]], clamped[:, pieces[k]], FUNC.Exp, bias=beta_sb[:, CORE : CORE + 1], scale=2.0
+            nc.vector.tensor_scalar(
+                clamped[:, pieces[k]], centred[:, pieces[k]], rstd[:, CORE : CORE + 1], ceiling[:], ALU.mult, ALU.min
             )
-        half_y = held.tile([P, N], F32, name="half_y")
+            nc.scalar.activation(expo[:, pieces[k]], clamped[:, pieces[k]], FUNC.Exp, bias=beta_c)
+        y_core = held.tile([P, N], F32, name="y_core")
+        log1p = held.tile([P, N], F32, name="log1p")
+        softplus = held.tile([P, N], F32, name="softplus")
         for k in range(NPIECE):
             nc.vector.tensor_scalar(
-                half_y[:, pieces[k]], centred[:, pieces[k]], scale_c[:], half_beta[:, CORE : CORE + 1], ALU.mult, ALU.add
+                y_core[:, pieces[k]], centred[:, pieces[k]], rstd[:, CORE : CORE + 1], beta_c, ALU.mult, ALU.add
             )
-
-        neg_mean_gamma = held.tile([P, 1], F32, name="neg_mean_gamma")
-        nc.vector.tensor_mul(neg_mean_gamma[:], moments[:, GATE, 0:1], neg_half_gamma[:, GATE : GATE + 1])
-        scale_g = held.tile([P, 1], F32, name="scale_g")
-        nc.vector.tensor_mul(scale_g[:], half_gamma[:, GATE : GATE + 1], rstd[:, GATE : GATE + 1])
-        shift_g = held.tile([P, 1], F32, name="shift_g")
-        nc.vector.tensor_scalar(
-            shift_g[:], neg_mean_gamma[:], rstd[:, GATE : GATE + 1], half_beta[:, GATE : GATE + 1], ALU.mult, ALU.add
-        )
-        tanh_g = held.tile([P, N], F32, name="tanh_g")
         for k in range(NPIECE):
-            nc.scalar.activation(tanh_g[:, pieces[k]], z[GATE, k][:], FUNC.Tanh, bias=shift_g[:], scale=scale_g[:])
+            nc.scalar.activation(log1p[:, pieces[k]], expo[:, pieces[k]], FUNC.Ln, bias=one[:])
+            nc.vector.tensor_max(softplus[:, pieces[k]], y_core[:, pieces[k]], log1p[:, pieces[k]])
 
-        log1p = held.tile([P, N], F32, name="log1p")
-        half_sp = held.tile([P, N], F32, name="half_sp")
+        normalise(GATE)
+        nc.vector.scalar_tensor_tensor(factors[:, 1:2], moments[:, GATE, 0:1], -1.0, factors[:, 0:1], ALU.mult, ALU.mult)
+        slope_offset = held.tile([P, 2], F32, name="slope_offset")
+        nc.vector.scalar_tensor_tensor(slope_offset[:], factors[:], rstd[:, GATE : GATE + 1], addends[:], ALU.mult, ALU.add)
+        sigmoid = held.tile([P, N], F32, name="sigmoid")
         prod = held.tile([P, N], F32, name="prod")
         out_sb = held.tile([P, S], F32, name="out_sb")
         for k in range(NPIECE):
-            nc.scalar.activation(log1p[:, pieces[k]], expo[:, pieces[k]], FUNC.Ln, bias=one[:])
-            nc.vector.scalar_tensor_tensor(
-                half_sp[:, pieces[k]], log1p[:, pieces[k]], 0.5, half_y[:, pieces[k]], ALU.mult, ALU.max
+            nc.scalar.activation(
+                sigmoid[:, pieces[k]], z[GATE, k][:], FUNC.Sigmoid, bias=slope_offset[:, 1:2], scale=slope_offset[:, 0:1]
             )
-            nc.vector.scalar_tensor_tensor(
-                prod[:, pieces[k]], tanh_g[:, pieces[k]], 1.0, half_sp[:, pieces[k]], ALU.add, ALU.mult
-            )
+            nc.vector.tensor_mul(prod[:, pieces[k]], sigmoid[:, pieces[k]], softplus[:, pieces[k]])
             nc.vector.tensor_reduce(
-                out_sb[:, k * ATOMS : (k + 1) * ATOMS],
+                out_sb[:, atoms[k]],
                 prod[:, pieces[k]].rearrange("p (i t) -> p i t", t=T),
                 axis=mybir.AxisListType.X,
                 op=ALU.add,

@@ -9,6 +9,7 @@ NPIECE = N // PIECE
 ATOMS = PIECE // T
 GATE, CORE = 0, 1
 CLAMP = 30.0
+WARM_UP = 2
 FLOPS = 2 * F * (N * D + S * D + N * E)
 
 BF16, F32, U16 = mybir.dt.bfloat16, mybir.dt.float32, mybir.dt.uint16
@@ -25,20 +26,25 @@ def tile_convlayer_kernel(tc, table, w_self, w_nbr, w_edge, edge, gamma1, beta1,
         tc.tile_pool(name="held", bufs=1) as held,
         tc.psum_pool(name="banks", bufs=8) as banks,
     ):
+        zeros = held.tile([P, 512], BF16, name="zeros")
+        nc.gpsimd.memset(zeros[:], 0.0)
+        unread = banks.tile([P, 512], F32, tag="bank", name="unread")
+        for turn in range(WARM_UP):
+            nc.tensor.matmul(unread[:], zeros[:, 0:P], zeros[:], start=True, stop=True)
+
         ident = held.tile([P, P], BF16, name="ident")
         make_identity(nc, ident[:])
         neg_half = held.tile([P, 1], F32, name="neg_half")
         nc.gpsimd.memset(neg_half[:], -0.5)
         one = held.tile([P, 1], F32, name="one")
-        nc.gpsimd.memset(one[:], 1.0)
+        nc.vector.memset(one[:], 1.0)
 
         rows = held.tile([P, S // P, D], BF16, name="rows")
         nc.sync.dma_start(rows[:], table.rearrange("(b p) d -> p b d", p=P))
         w_edge_sb = held.tile([P, F], BF16, name="w_edge_sb")
         nc.scalar.dma_start(w_edge_sb[:], w_edge)
         edge_sb = held.tile([P, N], BF16, name="edge_sb")
-        for k in range(NPIECE):
-            nc.scalar.dma_start(edge_sb[:, pieces[k]], edge[:, pieces[k]])
+        nc.scalar.dma_start(edge_sb[:], edge)
         w_self_sb = held.tile([P, F], BF16, name="w_self_sb")
         nc.sync.dma_start(w_self_sb[:], w_self)
         offsets = held.tile([P, N // 16], U16, name="offsets")
@@ -50,15 +56,17 @@ def tile_convlayer_kernel(tc, table, w_self, w_nbr, w_edge, edge, gamma1, beta1,
         with nc.allow_non_contiguous_dma(reason="one float to a partition, 256 in all"):
             nc.sync.dma_start(gamma_sb[:], gamma1.rearrange("(b p) o -> p (b o)", p=P))
             nc.sync.dma_start(beta_sb[:], beta1.rearrange("(b p) o -> p (b o)", p=P))
-        gamma_c, beta_c = gamma_sb[:, CORE : CORE + 1], beta_sb[:, CORE : CORE + 1]
+        beta_c = beta_sb[:, CORE : CORE + 1]
 
+        half_gamma = held.tile([P, 2], F32, name="half_gamma")
+        nc.vector.tensor_scalar_mul(half_gamma[:], gamma_sb[:], 0.5)
         ceiling = held.tile([P, 1], F32, name="ceiling")
-        nc.vector.tensor_scalar(ceiling[:], beta_c, -1.0, CLAMP, ALU.mult, ALU.add)
+        nc.vector.tensor_scalar(ceiling[:], beta_c, -0.5, CLAMP / 2, ALU.mult, ALU.add)
         factors = held.tile([P, 2], F32, name="factors")
-        nc.vector.tensor_copy(factors[:, 0:1], gamma_sb[:, GATE : GATE + 1])
+        nc.vector.tensor_scalar_mul(factors[:, 0:1], gamma_sb[:, GATE : GATE + 1], 0.5)
         addends = held.tile([P, 2], F32, name="addends")
         nc.vector.memset(addends[:, 0:1], 0.0)
-        nc.vector.tensor_copy(addends[:, 1:2], beta_sb[:, GATE : GATE + 1])
+        nc.vector.tensor_scalar_mul(addends[:, 1:2], beta_sb[:, GATE : GATE + 1], 0.5)
 
         flipped = banks.tile([P, S], BF16, tag="bank", name="flipped")
         for b in range(S // P):
@@ -109,47 +117,71 @@ def tile_convlayer_kernel(tc, table, w_self, w_nbr, w_edge, edge, gamma1, beta1,
             nc.gpsimd.tensor_tensor(rstd[:, blk : blk + 1], moments[:, blk, 1:2], neg_half[:], ALU.pow)
 
         normalise(CORE)
+        rstd_c = rstd[:, CORE : CORE + 1]
         neg_mean_gamma = held.tile([P, 1], F32, name="neg_mean_gamma")
-        nc.vector.scalar_tensor_tensor(neg_mean_gamma[:], moments[:, CORE, 0:1], -1.0, gamma_c, ALU.mult, ALU.mult)
+        nc.vector.scalar_tensor_tensor(
+            neg_mean_gamma[:], moments[:, CORE, 0:1], -1.0, half_gamma[:, CORE : CORE + 1], ALU.mult, ALU.mult
+        )
         centred = held.tile([P, N], F32, name="centred")
         for k in range(NPIECE):
-            nc.scalar.activation(centred[:, pieces[k]], z[CORE, k][:], FUNC.Identity, bias=neg_mean_gamma[:], scale=gamma_c)
+            nc.scalar.activation(
+                centred[:, pieces[k]],
+                z[CORE, k][:],
+                FUNC.Identity,
+                bias=neg_mean_gamma[:],
+                scale=half_gamma[:, CORE : CORE + 1],
+            )
         clamped = held.tile([P, N], F32, name="clamped")
         expo = held.tile([P, N], F32, name="expo")
         for k in range(NPIECE):
-            nc.vector.tensor_scalar(
-                clamped[:, pieces[k]], centred[:, pieces[k]], rstd[:, CORE : CORE + 1], ceiling[:], ALU.mult, ALU.min
-            )
-            nc.scalar.activation(expo[:, pieces[k]], clamped[:, pieces[k]], FUNC.Exp, bias=beta_c)
-        y_core = held.tile([P, N], F32, name="y_core")
-        log1p = held.tile([P, N], F32, name="log1p")
-        softplus = held.tile([P, N], F32, name="softplus")
-        for k in range(NPIECE):
-            nc.vector.tensor_scalar(
-                y_core[:, pieces[k]], centred[:, pieces[k]], rstd[:, CORE : CORE + 1], beta_c, ALU.mult, ALU.add
-            )
-        for k in range(NPIECE):
-            nc.scalar.activation(log1p[:, pieces[k]], expo[:, pieces[k]], FUNC.Ln, bias=one[:])
-            nc.vector.tensor_max(softplus[:, pieces[k]], y_core[:, pieces[k]], log1p[:, pieces[k]])
+            nc.vector.tensor_scalar(clamped[:, pieces[k]], centred[:, pieces[k]], rstd_c, ceiling[:], ALU.mult, ALU.min)
+            nc.scalar.activation(expo[:, pieces[k]], clamped[:, pieces[k]], FUNC.Exp, bias=beta_c, scale=2.0)
 
         normalise(GATE)
         nc.vector.scalar_tensor_tensor(factors[:, 1:2], moments[:, GATE, 0:1], -1.0, factors[:, 0:1], ALU.mult, ALU.mult)
         slope_offset = held.tile([P, 2], F32, name="slope_offset")
         nc.vector.scalar_tensor_tensor(slope_offset[:], factors[:], rstd[:, GATE : GATE + 1], addends[:], ALU.mult, ALU.add)
-        sigmoid = held.tile([P, N], F32, name="sigmoid")
-        prod = held.tile([P, N], F32, name="prod")
-        out_sb = held.tile([P, S], F32, name="out_sb")
+        tanh_g = held.tile([P, N], F32, name="tanh_g")
         for k in range(NPIECE):
             nc.scalar.activation(
-                sigmoid[:, pieces[k]], z[GATE, k][:], FUNC.Sigmoid, bias=slope_offset[:, 1:2], scale=slope_offset[:, 0:1]
+                tanh_g[:, pieces[k]], z[GATE, k][:], FUNC.Tanh, bias=slope_offset[:, 1:2], scale=slope_offset[:, 0:1]
             )
-            nc.vector.tensor_mul(prod[:, pieces[k]], sigmoid[:, pieces[k]], softplus[:, pieces[k]])
+
+        excess = held.tile([P, N], F32, tag="excess_then_log", name="excess")
+        for k in range(NPIECE):
+            nc.vector.scalar_tensor_tensor(
+                excess[:, pieces[k]], centred[:, pieces[k]], rstd_c, clamped[:, pieces[k]], ALU.mult, ALU.subtract
+            )
+        gated_excess = held.tile([P, N], F32, name="gated_excess")
+        early = held.tile([P, S], F32, name="early")
+        for k in range(NPIECE):
+            nc.vector.scalar_tensor_tensor(
+                gated_excess[:, pieces[k]], tanh_g[:, pieces[k]], 1.0, excess[:, pieces[k]], ALU.add, ALU.mult
+            )
+        for k in range(NPIECE):
             nc.vector.tensor_reduce(
-                out_sb[:, atoms[k]],
-                prod[:, pieces[k]].rearrange("p (i t) -> p i t", t=T),
+                early[:, atoms[k]],
+                gated_excess[:, pieces[k]].rearrange("p (i t) -> p i t", t=T),
+                axis=mybir.AxisListType.X,
+                op=ALU.add,
+            )
+
+        log1p = held.tile([P, N], F32, tag="excess_then_log", name="log1p")
+        gated_log = held.tile([P, N], F32, name="gated_log")
+        late = held.tile([P, S], F32, name="late")
+        out_sb = held.tile([P, S], F32, name="out_sb")
+        for k in range(NPIECE):
+            nc.scalar.activation(log1p[:, pieces[k]], expo[:, pieces[k]], FUNC.Ln, bias=one[:])
+            nc.vector.scalar_tensor_tensor(
+                gated_log[:, pieces[k]], tanh_g[:, pieces[k]], 1.0, log1p[:, pieces[k]], ALU.add, ALU.mult
+            )
+            nc.vector.tensor_reduce(
+                late[:, atoms[k]],
+                gated_log[:, pieces[k]].rearrange("p (i t) -> p i t", t=T),
                 axis=mybir.AxisListType.X,
                 op=ALU.add,
             )
             if k % 2 == 1:
                 half = slice((k - 1) * ATOMS, (k + 1) * ATOMS)
+                nc.vector.scalar_tensor_tensor(out_sb[:, half], late[:, half], 0.5, early[:, half], ALU.mult, ALU.add)
                 nc.sync.dma_start(out[:, half], out_sb[:, half])

@@ -9,6 +9,7 @@ NPIECE = N // PIECE
 ATOMS = PIECE // T
 GATE, CORE = 0, 1
 CLAMP = 30.0
+EXP_CLAMP = 1.0686474581524463e13
 WARM_UP = 2
 FLOPS = 2 * F * (N * D + S * D + N * E)
 
@@ -56,17 +57,15 @@ def tile_convlayer_kernel(tc, table, w_self, w_nbr, w_edge, edge, gamma1, beta1,
         with nc.allow_non_contiguous_dma(reason="one float to a partition, 256 in all"):
             nc.sync.dma_start(gamma_sb[:], gamma1.rearrange("(b p) o -> p (b o)", p=P))
             nc.sync.dma_start(beta_sb[:], beta1.rearrange("(b p) o -> p (b o)", p=P))
-        beta_c = beta_sb[:, CORE : CORE + 1]
 
-        half_gamma = held.tile([P, 2], F32, name="half_gamma")
-        nc.vector.tensor_scalar_mul(half_gamma[:], gamma_sb[:], 0.5)
-        ceiling = held.tile([P, 1], F32, name="ceiling")
-        nc.vector.tensor_scalar(ceiling[:], beta_c, -0.5, CLAMP / 2, ALU.mult, ALU.add)
-        factors = held.tile([P, 2], F32, name="factors")
-        nc.vector.tensor_scalar_mul(factors[:, 0:1], gamma_sb[:, GATE : GATE + 1], 0.5)
-        addends = held.tile([P, 2], F32, name="addends")
-        nc.vector.memset(addends[:, 0:1], 0.0)
-        nc.vector.tensor_scalar_mul(addends[:, 1:2], beta_sb[:, GATE : GATE + 1], 0.5)
+        factors = held.tile([P, 2, 2, 2], F32, name="factors")
+        neg_gamma = held.tile([P, 2, 2], F32, name="neg_gamma")
+        addends = held.tile([P, 2, 2, 2], F32, name="addends")
+        nc.vector.memset(addends[:, :, 0, :], 0.0)
+        for half, weight in enumerate((1.0, 0.5)):
+            nc.vector.tensor_scalar_mul(factors[:, :, 0, half], gamma_sb[:], weight)
+            nc.vector.tensor_scalar_mul(neg_gamma[:, :, half], gamma_sb[:], -weight)
+            nc.vector.tensor_scalar_mul(addends[:, :, 1, half], beta_sb[:], weight)
 
         flipped = banks.tile([P, S], BF16, tag="bank", name="flipped")
         for b in range(S // P):
@@ -108,80 +107,66 @@ def tile_convlayer_kernel(tc, table, w_self, w_nbr, w_edge, edge, gamma1, beta1,
         moments = held.tile([P, 2, 2], F32, name="moments")
         rstd = held.tile([P, 2], F32, name="rstd")
 
-        def normalise(blk):
+        def normalise(blk, affine):
             for k in range(NPIECE):
                 nc.vector.bn_stats(stats[:, blk, k, :], z[blk, k][:])
                 if k == 0:
                     nc.vector.tensor_scalar_add(stats[:, blk, 0, 2:3], stats[:, blk, 0, 2:3], N * EPS)
             nc.vector.bn_aggr(moments[:, blk, :], stats[:, blk, :, :])
             nc.gpsimd.tensor_tensor(rstd[:, blk : blk + 1], moments[:, blk, 1:2], neg_half[:], ALU.pow)
+            nc.vector.tensor_scalar_mul(factors[:, blk, 1, :], neg_gamma[:, blk, :], moments[:, blk, 0:1])
+            nc.vector.scalar_tensor_tensor(
+                affine[:],
+                factors[:, blk, :, :].rearrange("p a b -> p (a b)"),
+                rstd[:, blk : blk + 1],
+                addends[:, blk, :, :].rearrange("p a b -> p (a b)"),
+                ALU.mult,
+                ALU.add,
+            )
 
-        normalise(CORE)
-        rstd_c = rstd[:, CORE : CORE + 1]
-        neg_mean_gamma = held.tile([P, 1], F32, name="neg_mean_gamma")
-        nc.vector.scalar_tensor_tensor(
-            neg_mean_gamma[:], moments[:, CORE, 0:1], -1.0, half_gamma[:, CORE : CORE + 1], ALU.mult, ALU.mult
-        )
-        centred = held.tile([P, N], F32, name="centred")
+        SLOPE, HALF_SLOPE, OFFSET, HALF_OFFSET = [slice(i, i + 1) for i in range(4)]
+
+        affine_c = held.tile([P, 4], F32, name="affine_c")
+        normalise(CORE, affine_c)
+        expo = held.tile([P, N], F32, name="expo")
+        half_y = held.tile([P, N], F32, name="half_y")
+        for k in range(NPIECE):
+            nc.scalar.activation(expo[:, pieces[k]], z[CORE, k][:], FUNC.Exp, bias=affine_c[:, OFFSET], scale=affine_c[:, SLOPE])
         for k in range(NPIECE):
             nc.scalar.activation(
-                centred[:, pieces[k]],
-                z[CORE, k][:],
-                FUNC.Identity,
-                bias=neg_mean_gamma[:],
-                scale=half_gamma[:, CORE : CORE + 1],
+                half_y[:, pieces[k]], z[CORE, k][:], FUNC.Identity, bias=affine_c[:, HALF_OFFSET], scale=affine_c[:, HALF_SLOPE]
             )
-        clamped = held.tile([P, N], F32, name="clamped")
-        expo = held.tile([P, N], F32, name="expo")
-        for k in range(NPIECE):
-            nc.vector.tensor_scalar(clamped[:, pieces[k]], centred[:, pieces[k]], rstd_c, ceiling[:], ALU.mult, ALU.min)
-            nc.scalar.activation(expo[:, pieces[k]], clamped[:, pieces[k]], FUNC.Exp, bias=beta_c, scale=2.0)
 
-        normalise(GATE)
-        nc.vector.scalar_tensor_tensor(factors[:, 1:2], moments[:, GATE, 0:1], -1.0, factors[:, 0:1], ALU.mult, ALU.mult)
-        slope_offset = held.tile([P, 2], F32, name="slope_offset")
-        nc.vector.scalar_tensor_tensor(slope_offset[:], factors[:], rstd[:, GATE : GATE + 1], addends[:], ALU.mult, ALU.add)
+        affine_g = held.tile([P, 4], F32, tag="gate_then_log", name="affine_g")
+        normalise(GATE, affine_g)
         tanh_g = held.tile([P, N], F32, name="tanh_g")
         for k in range(NPIECE):
             nc.scalar.activation(
-                tanh_g[:, pieces[k]], z[GATE, k][:], FUNC.Tanh, bias=slope_offset[:, 1:2], scale=slope_offset[:, 0:1]
+                tanh_g[:, pieces[k]], z[GATE, k][:], FUNC.Tanh, bias=affine_g[:, HALF_OFFSET], scale=affine_g[:, HALF_SLOPE]
             )
 
-        excess = held.tile([P, N], F32, tag="excess_then_log", name="excess")
+        capped = held.tile([P, N], F32, name="capped")
         for k in range(NPIECE):
-            nc.vector.scalar_tensor_tensor(
-                excess[:, pieces[k]], centred[:, pieces[k]], rstd_c, clamped[:, pieces[k]], ALU.mult, ALU.subtract
-            )
-        gated_excess = held.tile([P, N], F32, name="gated_excess")
-        early = held.tile([P, S], F32, name="early")
-        for k in range(NPIECE):
-            nc.vector.scalar_tensor_tensor(
-                gated_excess[:, pieces[k]], tanh_g[:, pieces[k]], 1.0, excess[:, pieces[k]], ALU.add, ALU.mult
-            )
-        for k in range(NPIECE):
-            nc.vector.tensor_reduce(
-                early[:, atoms[k]],
-                gated_excess[:, pieces[k]].rearrange("p (i t) -> p i t", t=T),
-                axis=mybir.AxisListType.X,
-                op=ALU.add,
-            )
+            nc.vector.tensor_scalar_min(capped[:, pieces[k]], expo[:, pieces[k]], EXP_CLAMP)
 
-        log1p = held.tile([P, N], F32, tag="excess_then_log", name="log1p")
-        gated_log = held.tile([P, N], F32, name="gated_log")
-        late = held.tile([P, S], F32, name="late")
+        log1p = held.tile([P, N], F32, tag="gate_then_log", name="log1p")
+        half_sp = held.tile([P, N], F32, name="half_sp")
+        prod = held.tile([P, N], F32, name="prod")
         out_sb = held.tile([P, S], F32, name="out_sb")
         for k in range(NPIECE):
-            nc.scalar.activation(log1p[:, pieces[k]], expo[:, pieces[k]], FUNC.Ln, bias=one[:])
+            nc.scalar.activation(log1p[:, pieces[k]], capped[:, pieces[k]], FUNC.Ln, bias=one[:])
             nc.vector.scalar_tensor_tensor(
-                gated_log[:, pieces[k]], tanh_g[:, pieces[k]], 1.0, log1p[:, pieces[k]], ALU.add, ALU.mult
+                half_sp[:, pieces[k]], log1p[:, pieces[k]], 0.5, half_y[:, pieces[k]], ALU.mult, ALU.max
+            )
+            nc.vector.scalar_tensor_tensor(
+                prod[:, pieces[k]], tanh_g[:, pieces[k]], 1.0, half_sp[:, pieces[k]], ALU.add, ALU.mult
             )
             nc.vector.tensor_reduce(
-                late[:, atoms[k]],
-                gated_log[:, pieces[k]].rearrange("p (i t) -> p i t", t=T),
+                out_sb[:, atoms[k]],
+                prod[:, pieces[k]].rearrange("p (i t) -> p i t", t=T),
                 axis=mybir.AxisListType.X,
                 op=ALU.add,
             )
             if k % 2 == 1:
-                half = slice((k - 1) * ATOMS, (k + 1) * ATOMS)
-                nc.vector.scalar_tensor_tensor(out_sb[:, half], late[:, half], 0.5, early[:, half], ALU.mult, ALU.add)
-                nc.sync.dma_start(out[:, half], out_sb[:, half])
+                done = slice((k - 1) * ATOMS, (k + 1) * ATOMS)
+                nc.sync.dma_start(out[:, done], out_sb[:, done])

@@ -66,6 +66,7 @@ def tile_convlayer_kernel(tc, table, w_self, w_nbr, w_edge, edge, gamma1, beta1,
             nc.vector.tensor_scalar_mul(factors[:, :, 0, half], gamma_sb[:], weight)
             nc.vector.tensor_scalar_mul(neg_gamma[:, :, half], gamma_sb[:], -weight)
             nc.vector.tensor_scalar_mul(addends[:, :, 1, half], beta_sb[:], weight)
+        nc.vector.tensor_scalar_add(addends[:, CORE, 1, 1:2], addends[:, CORE, 1, 1:2], -CLAMP / 2)
 
         flipped = banks.tile([P, S], BF16, tag="bank", name="flipped")
         for b in range(S // P):
@@ -129,12 +130,12 @@ def tile_convlayer_kernel(tc, table, w_self, w_nbr, w_edge, edge, gamma1, beta1,
         affine_c = held.tile([P, 4], F32, name="affine_c")
         normalise(CORE, affine_c)
         expo = held.tile([P, N], F32, name="expo")
-        half_y = held.tile([P, N], F32, name="half_y")
+        excess = held.tile([P, N], F32, name="excess")
         for k in range(NPIECE):
             nc.scalar.activation(expo[:, pieces[k]], z[CORE, k][:], FUNC.Exp, bias=affine_c[:, OFFSET], scale=affine_c[:, SLOPE])
         for k in range(NPIECE):
             nc.scalar.activation(
-                half_y[:, pieces[k]], z[CORE, k][:], FUNC.Identity, bias=affine_c[:, HALF_OFFSET], scale=affine_c[:, HALF_SLOPE]
+                excess[:, pieces[k]], z[CORE, k][:], FUNC.Relu, bias=affine_c[:, HALF_OFFSET], scale=affine_c[:, HALF_SLOPE]
             )
 
         affine_g = held.tile([P, 4], F32, tag="gate_then_log", name="affine_g")
@@ -149,24 +150,36 @@ def tile_convlayer_kernel(tc, table, w_self, w_nbr, w_edge, edge, gamma1, beta1,
         for k in range(NPIECE):
             nc.vector.tensor_scalar_min(capped[:, pieces[k]], expo[:, pieces[k]], EXP_CLAMP)
 
+        gated_excess = held.tile([P, N], F32, name="gated_excess")
+        early = held.tile([P, S], F32, name="early")
+        for k in range(NPIECE):
+            nc.vector.scalar_tensor_tensor(
+                gated_excess[:, pieces[k]], tanh_g[:, pieces[k]], 1.0, excess[:, pieces[k]], ALU.add, ALU.mult
+            )
+        for k in range(NPIECE):
+            nc.vector.tensor_reduce(
+                early[:, atoms[k]],
+                gated_excess[:, pieces[k]].rearrange("p (i t) -> p i t", t=T),
+                axis=mybir.AxisListType.X,
+                op=ALU.add,
+            )
+
         log1p = held.tile([P, N], F32, tag="gate_then_log", name="log1p")
-        half_sp = held.tile([P, N], F32, name="half_sp")
-        prod = held.tile([P, N], F32, name="prod")
+        gated_log = held.tile([P, N], F32, name="gated_log")
+        late = held.tile([P, S], F32, name="late")
         out_sb = held.tile([P, S], F32, name="out_sb")
         for k in range(NPIECE):
             nc.scalar.activation(log1p[:, pieces[k]], capped[:, pieces[k]], FUNC.Ln, bias=one[:])
             nc.vector.scalar_tensor_tensor(
-                half_sp[:, pieces[k]], log1p[:, pieces[k]], 0.5, half_y[:, pieces[k]], ALU.mult, ALU.max
-            )
-            nc.vector.scalar_tensor_tensor(
-                prod[:, pieces[k]], tanh_g[:, pieces[k]], 1.0, half_sp[:, pieces[k]], ALU.add, ALU.mult
+                gated_log[:, pieces[k]], tanh_g[:, pieces[k]], 1.0, log1p[:, pieces[k]], ALU.add, ALU.mult
             )
             nc.vector.tensor_reduce(
-                out_sb[:, atoms[k]],
-                prod[:, pieces[k]].rearrange("p (i t) -> p i t", t=T),
+                late[:, atoms[k]],
+                gated_log[:, pieces[k]].rearrange("p (i t) -> p i t", t=T),
                 axis=mybir.AxisListType.X,
                 op=ALU.add,
             )
             if k % 2 == 1:
                 done = slice((k - 1) * ATOMS, (k + 1) * ATOMS)
+                nc.vector.scalar_tensor_tensor(out_sb[:, done], late[:, done], 0.5, early[:, done], ALU.mult, ALU.add)
                 nc.sync.dma_start(out[:, done], out_sb[:, done])

@@ -43,9 +43,9 @@ def tile_convlayer_kernel(tc, table, w_self, w_nbr, w_edge, edge, gamma1, beta1,
         rows = held.tile([P, S // P, D], BF16, name="rows")
         nc.sync.dma_start(rows[:], table.rearrange("(b p) d -> p b d", p=P))
         w_edge_sb = held.tile([P, F], BF16, name="w_edge_sb")
-        nc.scalar.dma_start(w_edge_sb[:], w_edge)
+        nc.sync.dma_start(w_edge_sb[:], w_edge)
         edge_sb = held.tile([P, N], BF16, name="edge_sb")
-        nc.scalar.dma_start(edge_sb[:], edge)
+        nc.sync.dma_start(edge_sb[:], edge)
         w_self_sb = held.tile([P, F], BF16, name="w_self_sb")
         nc.sync.dma_start(w_self_sb[:], w_self)
         offsets = held.tile([P, N // 16], U16, name="offsets")
@@ -55,8 +55,8 @@ def tile_convlayer_kernel(tc, table, w_self, w_nbr, w_edge, edge, gamma1, beta1,
         gamma_sb = held.tile([P, 2], F32, name="gamma_sb")
         beta_sb = held.tile([P, 2], F32, name="beta_sb")
         with nc.allow_non_contiguous_dma(reason="one float to a partition, 256 in all"):
-            nc.sync.dma_start(gamma_sb[:], gamma1.rearrange("(b p) o -> p (b o)", p=P))
-            nc.sync.dma_start(beta_sb[:], beta1.rearrange("(b p) o -> p (b o)", p=P))
+            nc.scalar.dma_start(gamma_sb[:], gamma1.rearrange("(b p) o -> p (b o)", p=P))
+            nc.scalar.dma_start(beta_sb[:], beta1.rearrange("(b p) o -> p (b o)", p=P))
 
         factors = held.tile([P, 2, 2, 2], F32, name="factors")
         neg_gamma = held.tile([P, 2, 2], F32, name="neg_gamma")

@@ -44,8 +44,9 @@ def tile_convlayer_kernel(tc, table, w_self, w_nbr, w_edge, edge, gamma1, beta1,
         nc.sync.dma_start(rows[:], table.rearrange("(b p) d -> p b d", p=P))
         w_edge_sb = held.tile([P, F], BF16, name="w_edge_sb")
         nc.sync.dma_start(w_edge_sb[:], w_edge)
-        edge_sb = held.tile([P, N], BF16, name="edge_sb")
-        nc.sync.dma_start(edge_sb[:], edge)
+        edge_sb = [held.tile([P, N // 2], BF16, name=f"edge_sb{h}") for h in range(2)]
+        for h in range(2):
+            nc.sync.dma_start(edge_sb[h][:], edge[:, h * (N // 2) : (h + 1) * (N // 2)])
         w_self_sb = held.tile([P, F], BF16, name="w_self_sb")
         nc.sync.dma_start(w_self_sb[:], w_self)
         offsets = held.tile([P, N // 16], U16, name="offsets")
@@ -80,7 +81,7 @@ def tile_convlayer_kernel(tc, table, w_self, w_nbr, w_edge, edge, gamma1, beta1,
                 z[blk, k] = banks.tile([P, PIECE], F32, tag="bank", name=f"z{blk}_{k}")
 
         def edge_product(blk, k, start, stop):
-            nc.tensor.matmul(z[blk, k][:], w_edge_sb[:, features[blk]], edge_sb[:, pieces[k]], start=start, stop=stop)
+            nc.tensor.matmul(z[blk, k][:], w_edge_sb[:, features[blk]], edge_sb[k // 2][:, pieces[k % 2]], start=start, stop=stop)
 
         def own_product(blk, k, start, stop):
             own = tab_t[:, atoms[k]].unsqueeze(2).to_broadcast([P, ATOMS, T])

@@ -9,7 +9,6 @@ NPIECE = N // PIECE
 ATOMS = PIECE // T
 GATE, CORE = 0, 1
 CLAMP = 30.0
-EXP_CLAMP = 1.0686474581524463e13
 WARM_UP = 2
 FLOPS = 2 * F * (N * D + S * D + N * E)
 
@@ -39,6 +38,8 @@ def tile_convlayer_kernel(tc, table, w_self, w_nbr, w_edge, edge, gamma1, beta1,
         nc.gpsimd.memset(neg_half[:], -0.5)
         one = held.tile([P, 1], F32, name="one")
         nc.vector.memset(one[:], 1.0)
+        exp_clamp = held.tile([P, 1], F32, name="exp_clamp")
+        nc.scalar.activation(exp_clamp[:], one[:], FUNC.Exp, scale=CLAMP)
 
         rows = held.tile([P, S // P, D], BF16, name="rows")
         nc.sync.dma_start(rows[:], table.rearrange("(b p) d -> p b d", p=P))
@@ -67,6 +68,9 @@ def tile_convlayer_kernel(tc, table, w_self, w_nbr, w_edge, edge, gamma1, beta1,
             nc.vector.tensor_scalar_mul(factors[:, :, 0, half], gamma_sb[:], weight)
             nc.vector.tensor_scalar_mul(neg_gamma[:, :, half], gamma_sb[:], -weight)
             nc.vector.tensor_scalar_mul(addends[:, :, 1, half], beta_sb[:], weight)
+        signed_gamma_c = held.tile([P, 4], F32, name="signed_gamma_c")
+        for i, weight in enumerate((1.0, 0.5, -1.0, -0.5)):
+            nc.vector.tensor_scalar_mul(signed_gamma_c[:, i : i + 1], gamma_sb[:, CORE : CORE + 1], weight)
         nc.vector.tensor_scalar_add(addends[:, CORE, 1, 1:2], addends[:, CORE, 1, 1:2], -CLAMP / 2)
 
         flipped = banks.tile([P, S], BF16, tag="bank", name="flipped")
@@ -109,38 +113,46 @@ def tile_convlayer_kernel(tc, table, w_self, w_nbr, w_edge, edge, gamma1, beta1,
         moments = held.tile([P, 2, 2], F32, name="moments")
         rstd = held.tile([P, 2], F32, name="rstd")
 
-        def normalise(blk, affine):
+        def measure(blk):
             for k in range(NPIECE):
                 nc.vector.bn_stats(stats[:, blk, k, :], z[blk, k][:])
                 if k == 0:
                     nc.vector.tensor_scalar_add(stats[:, blk, 0, 2:3], stats[:, blk, 0, 2:3], N * EPS)
             nc.vector.bn_aggr(moments[:, blk, :], stats[:, blk, :, :])
             nc.gpsimd.tensor_tensor(rstd[:, blk : blk + 1], moments[:, blk, 1:2], neg_half[:], ALU.pow)
-            nc.vector.tensor_scalar_mul(factors[:, blk, 1, :], neg_gamma[:, blk, :], moments[:, blk, 0:1])
-            nc.vector.scalar_tensor_tensor(
-                affine[:],
-                factors[:, blk, :, :].rearrange("p a b -> p (a b)"),
-                rstd[:, blk : blk + 1],
-                addends[:, blk, :, :].rearrange("p a b -> p (a b)"),
-                ALU.mult,
-                ALU.add,
-            )
 
         SLOPE, HALF_SLOPE, OFFSET, HALF_OFFSET = [slice(i, i + 1) for i in range(4)]
 
-        affine_c = held.tile([P, 4], F32, name="affine_c")
-        normalise(CORE, affine_c)
+        measure(CORE)
+        slopes_c = held.tile([P, 4], F32, name="slopes_c")
+        nc.scalar.activation(slopes_c[:], signed_gamma_c[:], FUNC.Identity, scale=rstd[:, CORE : CORE + 1])
+        offsets_c = held.tile([P, 2], F32, name="offsets_c")
+        for half in range(2):
+            nc.scalar.activation(
+                offsets_c[:, half : half + 1],
+                moments[:, CORE, 0:1],
+                FUNC.Identity,
+                bias=addends[:, CORE, 1, half : half + 1],
+                scale=slopes_c[:, 2 + half : 3 + half],
+            )
         expo = held.tile([P, N], F32, name="expo")
         excess = held.tile([P, N], F32, name="excess")
         for k in range(NPIECE):
-            nc.scalar.activation(expo[:, pieces[k]], z[CORE, k][:], FUNC.Exp, bias=affine_c[:, OFFSET], scale=affine_c[:, SLOPE])
+            nc.scalar.activation(expo[:, pieces[k]], z[CORE, k][:], FUNC.Exp, bias=offsets_c[:, 0:1], scale=slopes_c[:, 0:1])
         for k in range(NPIECE):
-            nc.scalar.activation(
-                excess[:, pieces[k]], z[CORE, k][:], FUNC.Relu, bias=affine_c[:, HALF_OFFSET], scale=affine_c[:, HALF_SLOPE]
-            )
+            nc.scalar.activation(excess[:, pieces[k]], z[CORE, k][:], FUNC.Relu, bias=offsets_c[:, 1:2], scale=slopes_c[:, 1:2])
 
+        measure(GATE)
         affine_g = held.tile([P, 4], F32, tag="gate_then_log", name="affine_g")
-        normalise(GATE, affine_g)
+        nc.vector.tensor_scalar_mul(factors[:, GATE, 1, :], neg_gamma[:, GATE, :], moments[:, GATE, 0:1])
+        nc.vector.scalar_tensor_tensor(
+            affine_g[:],
+            factors[:, GATE, :, :].rearrange("p a b -> p (a b)"),
+            rstd[:, GATE : GATE + 1],
+            addends[:, GATE, :, :].rearrange("p a b -> p (a b)"),
+            ALU.mult,
+            ALU.add,
+        )
         tanh_g = held.tile([P, N], F32, name="tanh_g")
         for k in range(NPIECE):
             nc.scalar.activation(
@@ -149,7 +161,7 @@ def tile_convlayer_kernel(tc, table, w_self, w_nbr, w_edge, edge, gamma1, beta1,
 
         capped = held.tile([P, N], F32, name="capped")
         for k in range(NPIECE):
-            nc.vector.tensor_scalar_min(capped[:, pieces[k]], expo[:, pieces[k]], EXP_CLAMP)
+            nc.vector.tensor_scalar_min(capped[:, pieces[k]], expo[:, pieces[k]], exp_clamp[:])
 
         gated_excess = held.tile([P, N], F32, name="gated_excess")
         early = held.tile([P, S], F32, name="early")

@@ -9,7 +9,7 @@ NPIECE = N // PIECE
 ATOMS = PIECE // T
 GATE, CORE = 0, 1
 CLAMP = 30.0
-WARM_UP = 2
+WARM_UP = 4
 FLOPS = 2 * F * (N * D + S * D + N * E)
 
 BF16, F32, U16 = mybir.dt.bfloat16, mybir.dt.float32, mybir.dt.uint16
@@ -26,11 +26,11 @@ def tile_convlayer_kernel(tc, table, w_self, w_nbr, w_edge, edge, gamma1, beta1,
         tc.tile_pool(name="held", bufs=1) as held,
         tc.psum_pool(name="banks", bufs=8) as banks,
     ):
-        zeros = held.tile([P, 512], BF16, name="zeros")
+        zeros = held.tile([P, 32], BF16, name="zeros")
         nc.gpsimd.memset(zeros[:], 0.0)
-        unread = banks.tile([P, 512], F32, tag="bank", name="unread")
+        unread = banks.tile([32, 16, 32], F32, tag="bank", name="unread")
         for turn in range(WARM_UP):
-            nc.tensor.matmul(unread[:], zeros[:, 0:P], zeros[:], start=True, stop=True)
+            nc.tensor.matmul(unread[:], zeros[:], zeros[:].unsqueeze(1).to_broadcast([P, 16, 32]), start=True, stop=True)
 
         ident = held.tile([P, P], BF16, name="ident")
         make_identity(nc, ident[:])
@@ -111,7 +111,7 @@ def tile_convlayer_kernel(tc, table, w_self, w_nbr, w_edge, edge, gamma1, beta1,
 
         stats = held.tile([P, 2, NPIECE, 6], F32, name="stats")
         moments = held.tile([P, 2, 2], F32, name="moments")
-        rstd = held.tile([P, 2], F32, name="rstd")
+        rstd = held.tile([P, 2], F32, tag="rstd_then_capped", name="rstd")
 
         def measure(blk):
             for k in range(NPIECE):
@@ -139,8 +139,11 @@ def tile_convlayer_kernel(tc, table, w_self, w_nbr, w_edge, edge, gamma1, beta1,
         excess = held.tile([P, N], F32, name="excess")
         for k in range(NPIECE):
             nc.scalar.activation(expo[:, pieces[k]], z[CORE, k][:], FUNC.Exp, bias=offsets_c[:, 0:1], scale=slopes_c[:, 0:1])
-        for k in range(NPIECE):
+        for k in range(NPIECE - 1):
             nc.scalar.activation(excess[:, pieces[k]], z[CORE, k][:], FUNC.Relu, bias=offsets_c[:, 1:2], scale=slopes_c[:, 1:2])
+        last = pieces[NPIECE - 1]
+        nc.vector.tensor_scalar(excess[:, last], z[CORE, NPIECE - 1][:], slopes_c[:, 1:2], offsets_c[:, 1:2], ALU.mult, ALU.add)
+        nc.vector.tensor_scalar_max(excess[:, last], excess[:, last], 0.0)
 
         measure(GATE)
         affine_g = held.tile([P, 4], F32, tag="gate_then_log", name="affine_g")
@@ -159,20 +162,23 @@ def tile_convlayer_kernel(tc, table, w_self, w_nbr, w_edge, edge, gamma1, beta1,
                 tanh_g[:, pieces[k]], z[GATE, k][:], FUNC.Tanh, bias=affine_g[:, HALF_OFFSET], scale=affine_g[:, HALF_SLOPE]
             )
 
-        capped = held.tile([P, N], F32, name="capped")
-        for k in range(NPIECE):
-            nc.vector.tensor_scalar_min(capped[:, pieces[k]], expo[:, pieces[k]], exp_clamp[:])
+        wide = [slice(h * 2 * PIECE, (h + 1) * 2 * PIECE) for h in range(NPIECE // 2)]
+        wide_atoms = [slice(h * 2 * ATOMS, (h + 1) * 2 * ATOMS) for h in range(NPIECE // 2)]
+
+        capped = held.tile([P, N], F32, tag="rstd_then_capped", name="capped")
+        for h in range(NPIECE // 2):
+            nc.vector.tensor_scalar_min(capped[:, wide[h]], expo[:, wide[h]], exp_clamp[:])
 
         gated_excess = held.tile([P, N], F32, name="gated_excess")
         early = held.tile([P, S], F32, name="early")
-        for k in range(NPIECE):
+        for h in range(NPIECE // 2):
             nc.vector.scalar_tensor_tensor(
-                gated_excess[:, pieces[k]], tanh_g[:, pieces[k]], 1.0, excess[:, pieces[k]], ALU.add, ALU.mult
+                gated_excess[:, wide[h]], tanh_g[:, wide[h]], 1.0, excess[:, wide[h]], ALU.add, ALU.mult
             )
-        for k in range(NPIECE):
+        for h in range(NPIECE // 2):
             nc.vector.tensor_reduce(
-                early[:, atoms[k]],
-                gated_excess[:, pieces[k]].rearrange("p (i t) -> p i t", t=T),
+                early[:, wide_atoms[h]],
+                gated_excess[:, wide[h]].rearrange("p (i t) -> p i t", t=T),
                 axis=mybir.AxisListType.X,
                 op=ALU.add,
             )
@@ -181,18 +187,17 @@ def tile_convlayer_kernel(tc, table, w_self, w_nbr, w_edge, edge, gamma1, beta1,
         gated_log = held.tile([P, N], F32, name="gated_log")
         late = held.tile([P, S], F32, name="late")
         out_sb = held.tile([P, S], F32, name="out_sb")
-        for k in range(NPIECE):
-            nc.scalar.activation(log1p[:, pieces[k]], capped[:, pieces[k]], FUNC.Ln, bias=one[:])
+        for h in range(NPIECE // 2):
+            nc.scalar.activation(log1p[:, wide[h]], capped[:, wide[h]], FUNC.Ln, bias=one[:])
             nc.vector.scalar_tensor_tensor(
-                gated_log[:, pieces[k]], tanh_g[:, pieces[k]], 1.0, log1p[:, pieces[k]], ALU.add, ALU.mult
+                gated_log[:, wide[h]], tanh_g[:, wide[h]], 1.0, log1p[:, wide[h]], ALU.add, ALU.mult
             )
             nc.vector.tensor_reduce(
-                late[:, atoms[k]],
-                gated_log[:, pieces[k]].rearrange("p (i t) -> p i t", t=T),
+                late[:, wide_atoms[h]],
+                gated_log[:, wide[h]].rearrange("p (i t) -> p i t", t=T),
                 axis=mybir.AxisListType.X,
                 op=ALU.add,
             )
-            if k % 2 == 1:
-                done = slice((k - 1) * ATOMS, (k + 1) * ATOMS)
-                nc.vector.scalar_tensor_tensor(out_sb[:, done], late[:, done], 0.5, early[:, done], ALU.mult, ALU.add)
-                nc.sync.dma_start(out[:, done], out_sb[:, done])
+            done = wide_atoms[h]
+            nc.vector.scalar_tensor_tensor(out_sb[:, done], late[:, done], 0.5, early[:, done], ALU.mult, ALU.add)
+            nc.sync.dma_start(out[:, done], out_sb[:, done])

@@ -38,8 +38,11 @@ def tile_convlayer_kernel(tc, table, w_self, w_nbr, w_edge, edge, gamma1, beta1,
         nc.gpsimd.memset(neg_half[:], -0.5)
         one = held.tile([P, 1], F32, name="one")
         nc.vector.memset(one[:], 1.0)
-        exp_clamp = held.tile([P, 1], F32, name="exp_clamp")
-        nc.scalar.activation(exp_clamp[:], one[:], FUNC.Exp, scale=CLAMP)
+        neg_half_clamp = held.tile([P, 1], F32, name="neg_half_clamp")
+        nc.vector.memset(neg_half_clamp[:], -CLAMP / 2)
+        signs_and_scales = held.tile([P, 4], F32, name="signs_and_scales")
+        for i, weight in enumerate((1.0, 0.5, -1.0, -0.5)):
+            nc.vector.memset(signs_and_scales[:, i : i + 1], weight)
 
         rows = held.tile([P, S // P, D], BF16, name="rows")
         nc.sync.dma_start(rows[:], table.rearrange("(b p) d -> p b d", p=P))
@@ -60,18 +63,20 @@ def tile_convlayer_kernel(tc, table, w_self, w_nbr, w_edge, edge, gamma1, beta1,
             nc.scalar.dma_start(gamma_sb[:], gamma1.rearrange("(b p) o -> p (b o)", p=P))
             nc.scalar.dma_start(beta_sb[:], beta1.rearrange("(b p) o -> p (b o)", p=P))
 
-        factors = held.tile([P, 2, 2, 2], F32, name="factors")
-        neg_gamma = held.tile([P, 2, 2], F32, name="neg_gamma")
-        addends = held.tile([P, 2, 2, 2], F32, name="addends")
-        nc.vector.memset(addends[:, :, 0, :], 0.0)
-        for half, weight in enumerate((1.0, 0.5)):
-            nc.vector.tensor_scalar_mul(factors[:, :, 0, half], gamma_sb[:], weight)
-            nc.vector.tensor_scalar_mul(neg_gamma[:, :, half], gamma_sb[:], -weight)
-            nc.vector.tensor_scalar_mul(addends[:, :, 1, half], beta_sb[:], weight)
+        exp_clamp = held.tile([P, 1], F32, name="exp_clamp")
+        nc.scalar.activation(exp_clamp[:], one[:], FUNC.Exp, scale=CLAMP)
+
         signed_gamma_c = held.tile([P, 4], F32, name="signed_gamma_c")
-        for i, weight in enumerate((1.0, 0.5, -1.0, -0.5)):
-            nc.vector.tensor_scalar_mul(signed_gamma_c[:, i : i + 1], gamma_sb[:, CORE : CORE + 1], weight)
-        nc.vector.tensor_scalar_add(addends[:, CORE, 1, 1:2], addends[:, CORE, 1, 1:2], -CLAMP / 2)
+        nc.scalar.activation(signed_gamma_c[:], signs_and_scales[:], FUNC.Identity, scale=gamma_sb[:, CORE : CORE + 1])
+        half_beta_c = held.tile([P, 1], F32, name="half_beta_c")
+        nc.scalar.activation(half_beta_c[:], beta_sb[:, CORE : CORE + 1], FUNC.Identity, bias=neg_half_clamp[:], scale=0.5)
+        factors_g = held.tile([P, 2], F32, name="factors_g")
+        nc.scalar.mul(factors_g[:, 0:1], gamma_sb[:, GATE : GATE + 1], 0.5)
+        neg_half_gamma_g = held.tile([P, 1], F32, name="neg_half_gamma_g")
+        nc.scalar.mul(neg_half_gamma_g[:], gamma_sb[:, GATE : GATE + 1], -0.5)
+        addends_g = held.tile([P, 2], F32, name="addends_g")
+        nc.vector.memset(addends_g[:, 0:1], 0.0)
+        nc.scalar.mul(addends_g[:, 1:2], beta_sb[:, GATE : GATE + 1], 0.5)
 
         flipped = banks.tile([P, S], BF16, tag="bank", name="flipped")
         for b in range(S // P):
@@ -121,18 +126,16 @@ def tile_convlayer_kernel(tc, table, w_self, w_nbr, w_edge, edge, gamma1, beta1,
             nc.vector.bn_aggr(moments[:, blk, :], stats[:, blk, :, :])
             nc.gpsimd.tensor_tensor(rstd[:, blk : blk + 1], moments[:, blk, 1:2], neg_half[:], ALU.pow)
 
-        SLOPE, HALF_SLOPE, OFFSET, HALF_OFFSET = [slice(i, i + 1) for i in range(4)]
-
         measure(CORE)
         slopes_c = held.tile([P, 4], F32, name="slopes_c")
         nc.scalar.activation(slopes_c[:], signed_gamma_c[:], FUNC.Identity, scale=rstd[:, CORE : CORE + 1])
         offsets_c = held.tile([P, 2], F32, name="offsets_c")
-        for half in range(2):
+        for half, addend in enumerate((beta_sb[:, CORE : CORE + 1], half_beta_c[:])):
             nc.scalar.activation(
                 offsets_c[:, half : half + 1],
                 moments[:, CORE, 0:1],
                 FUNC.Identity,
-                bias=addends[:, CORE, 1, half : half + 1],
+                bias=addend,
                 scale=slopes_c[:, 2 + half : 3 + half],
             )
         expo = held.tile([P, N], F32, name="expo")
@@ -146,21 +149,12 @@ def tile_convlayer_kernel(tc, table, w_self, w_nbr, w_edge, edge, gamma1, beta1,
         nc.vector.tensor_scalar_max(excess[:, last], excess[:, last], 0.0)
 
         measure(GATE)
-        affine_g = held.tile([P, 4], F32, tag="gate_then_log", name="affine_g")
-        nc.vector.tensor_scalar_mul(factors[:, GATE, 1, :], neg_gamma[:, GATE, :], moments[:, GATE, 0:1])
-        nc.vector.scalar_tensor_tensor(
-            affine_g[:],
-            factors[:, GATE, :, :].rearrange("p a b -> p (a b)"),
-            rstd[:, GATE : GATE + 1],
-            addends[:, GATE, :, :].rearrange("p a b -> p (a b)"),
-            ALU.mult,
-            ALU.add,
-        )
+        affine_g = held.tile([P, 2], F32, tag="gate_then_log", name="affine_g")
+        nc.vector.tensor_scalar_mul(factors_g[:, 1:2], neg_half_gamma_g[:], moments[:, GATE, 0:1])
+        nc.vector.scalar_tensor_tensor(affine_g[:], factors_g[:], rstd[:, GATE : GATE + 1], addends_g[:], ALU.mult, ALU.add)
         tanh_g = held.tile([P, N], F32, name="tanh_g")
         for k in range(NPIECE):
-            nc.scalar.activation(
-                tanh_g[:, pieces[k]], z[GATE, k][:], FUNC.Tanh, bias=affine_g[:, HALF_OFFSET], scale=affine_g[:, HALF_SLOPE]
-            )
+            nc.scalar.activation(tanh_g[:, pieces[k]], z[GATE, k][:], FUNC.Tanh, bias=affine_g[:, 1:2], scale=affine_g[:, 0:1])
 
         wide = [slice(h * 2 * PIECE, (h + 1) * 2 * PIECE) for h in range(NPIECE // 2)]
         wide_atoms = [slice(h * 2 * ATOMS, (h + 1) * 2 * ATOMS) for h in range(NPIECE // 2)]

@@ -142,11 +142,11 @@ def tile_convlayer_kernel(tc, table, w_self, w_nbr, w_edge, edge, gamma1, beta1,
         excess = held.tile([P, N], F32, name="excess")
         for k in range(NPIECE):
             nc.scalar.activation(expo[:, pieces[k]], z[CORE, k][:], FUNC.Exp, bias=offsets_c[:, 0:1], scale=slopes_c[:, 0:1])
-        for k in range(NPIECE - 1):
+        for k in range(NPIECE // 2):
             nc.scalar.activation(excess[:, pieces[k]], z[CORE, k][:], FUNC.Relu, bias=offsets_c[:, 1:2], scale=slopes_c[:, 1:2])
-        last = pieces[NPIECE - 1]
-        nc.vector.tensor_scalar(excess[:, last], z[CORE, NPIECE - 1][:], slopes_c[:, 1:2], offsets_c[:, 1:2], ALU.mult, ALU.add)
-        nc.vector.tensor_scalar_max(excess[:, last], excess[:, last], 0.0)
+        for k in range(NPIECE // 2, NPIECE):
+            nc.vector.tensor_scalar(excess[:, pieces[k]], z[CORE, k][:], slopes_c[:, 1:2], offsets_c[:, 1:2], ALU.mult, ALU.add)
+        nc.vector.tensor_scalar_max(excess[:, N // 2 : N], excess[:, N // 2 : N], 0.0)
 
         measure(GATE)
         affine_g = held.tile([P, 2], F32, tag="gate_then_log", name="affine_g")

@@ -158,27 +158,31 @@ def tile_convlayer_kernel(tc, table, w_self, w_nbr, w_edge, edge, gamma1, beta1,
 
         wide = [slice(h * 2 * PIECE, (h + 1) * 2 * PIECE) for h in range(NPIECE // 2)]
         wide_atoms = [slice(h * 2 * ATOMS, (h + 1) * 2 * ATOMS) for h in range(NPIECE // 2)]
+        wide_pairs = [slice(h * PIECE, (h + 1) * PIECE) for h in range(NPIECE // 2)]
+
+        def sum_over_bonds(sums, terms, pairs):
+            by_bond = terms.rearrange("p (i t) -> p i t", t=T)
+            by_pair = pairs.rearrange("p (i u) -> p i u", u=2)
+            nc.vector.tensor_tensor(by_pair, by_bond[:, :, 0:2], by_bond[:, :, 2:4], ALU.add)
+            nc.vector.tensor_tensor(sums, by_pair[:, :, 0], by_pair[:, :, 1], ALU.add)
 
         capped = held.tile([P, N], F32, tag="rstd_then_capped", name="capped")
         for h in range(NPIECE // 2):
             nc.vector.tensor_scalar_min(capped[:, wide[h]], expo[:, wide[h]], exp_clamp[:])
 
         gated_excess = held.tile([P, N], F32, name="gated_excess")
+        early_pairs = held.tile([P, N // 2], F32, name="early_pairs")
         early = held.tile([P, S], F32, name="early")
         for h in range(NPIECE // 2):
             nc.vector.scalar_tensor_tensor(
                 gated_excess[:, wide[h]], tanh_g[:, wide[h]], 1.0, excess[:, wide[h]], ALU.add, ALU.mult
             )
         for h in range(NPIECE // 2):
-            nc.vector.tensor_reduce(
-                early[:, wide_atoms[h]],
-                gated_excess[:, wide[h]].rearrange("p (i t) -> p i t", t=T),
-                axis=mybir.AxisListType.X,
-                op=ALU.add,
-            )
+            sum_over_bonds(early[:, wide_atoms[h]], gated_excess[:, wide[h]], early_pairs[:, wide_pairs[h]])
 
         log1p = held.tile([P, N], F32, tag="gate_then_log", name="log1p")
         gated_log = held.tile([P, N], F32, name="gated_log")
+        late_pairs = held.tile([P, N // 2], F32, name="late_pairs")
         late = held.tile([P, S], F32, name="late")
         out_sb = held.tile([P, S], F32, name="out_sb")
         for h in range(NPIECE // 2):
@@ -186,12 +190,7 @@ def tile_convlayer_kernel(tc, table, w_self, w_nbr, w_edge, edge, gamma1, beta1,
             nc.vector.scalar_tensor_tensor(
                 gated_log[:, wide[h]], tanh_g[:, wide[h]], 1.0, log1p[:, wide[h]], ALU.add, ALU.mult
             )
-            nc.vector.tensor_reduce(
-                late[:, wide_atoms[h]],
-                gated_log[:, wide[h]].rearrange("p (i t) -> p i t", t=T),
-                axis=mybir.AxisListType.X,
-                op=ALU.add,
-            )
+            sum_over_bonds(late[:, wide_atoms[h]], gated_log[:, wide[h]], late_pairs[:, wide_pairs[h]])
             done = wide_atoms[h]
             nc.vector.scalar_tensor_tensor(out_sb[:, done], late[:, done], 0.5, early[:, done], ALU.mult, ALU.add)
             nc.sync.dma_start(out[:, done], out_sb[:, done])

@@ -9,6 +9,7 @@ NPIECE = N // PIECE
 ATOMS = PIECE // T
 GATE, CORE = 0, 1
 CLAMP = 30.0
+SMALL = 1 / (2 * CLAMP)
 WARM_UP = 4
 FLOPS = 2 * F * (N * D + S * D + N * E)
 
@@ -38,10 +39,8 @@ def tile_convlayer_kernel(tc, table, w_self, w_nbr, w_edge, edge, gamma1, beta1,
         nc.gpsimd.memset(neg_half[:], -0.5)
         one = held.tile([P, 1], F32, name="one")
         nc.vector.memset(one[:], 1.0)
-        neg_half_clamp = held.tile([P, 1], F32, name="neg_half_clamp")
-        nc.vector.memset(neg_half_clamp[:], -CLAMP / 2)
         signs_and_scales = held.tile([P, 4], F32, name="signs_and_scales")
-        for i, weight in enumerate((1.0, 0.5, -1.0, -0.5)):
+        for i, weight in enumerate((1.0, SMALL, -1.0, -SMALL)):
             nc.vector.memset(signs_and_scales[:, i : i + 1], weight)
 
         rows = held.tile([P, S // P, D], BF16, name="rows")
@@ -68,8 +67,8 @@ def tile_convlayer_kernel(tc, table, w_self, w_nbr, w_edge, edge, gamma1, beta1,
 
         signed_gamma_c = held.tile([P, 4], F32, name="signed_gamma_c")
         nc.scalar.activation(signed_gamma_c[:], signs_and_scales[:], FUNC.Identity, scale=gamma_sb[:, CORE : CORE + 1])
-        half_beta_c = held.tile([P, 1], F32, name="half_beta_c")
-        nc.scalar.activation(half_beta_c[:], beta_sb[:, CORE : CORE + 1], FUNC.Identity, bias=neg_half_clamp[:], scale=0.5)
+        small_beta_c = held.tile([P, 1], F32, name="small_beta_c")
+        nc.scalar.mul(small_beta_c[:], beta_sb[:, CORE : CORE + 1], SMALL)
         factors_g = held.tile([P, 2], F32, name="factors_g")
         nc.scalar.mul(factors_g[:, 0:1], gamma_sb[:, GATE : GATE + 1], 0.5)
         neg_half_gamma_g = held.tile([P, 1], F32, name="neg_half_gamma_g")
@@ -130,23 +129,22 @@ def tile_convlayer_kernel(tc, table, w_self, w_nbr, w_edge, edge, gamma1, beta1,
         slopes_c = held.tile([P, 4], F32, name="slopes_c")
         nc.scalar.activation(slopes_c[:], signed_gamma_c[:], FUNC.Identity, scale=rstd[:, CORE : CORE + 1])
         offsets_c = held.tile([P, 2], F32, name="offsets_c")
-        for half, addend in enumerate((beta_sb[:, CORE : CORE + 1], half_beta_c[:])):
+        for line, addend in enumerate((beta_sb[:, CORE : CORE + 1], small_beta_c[:])):
             nc.scalar.activation(
-                offsets_c[:, half : half + 1],
+                offsets_c[:, line : line + 1],
                 moments[:, CORE, 0:1],
                 FUNC.Identity,
                 bias=addend,
-                scale=slopes_c[:, 2 + half : 3 + half],
+                scale=slopes_c[:, 2 + line : 3 + line],
             )
         expo = held.tile([P, N], F32, name="expo")
-        excess = held.tile([P, N], F32, name="excess")
+        ratio = held.tile([P, N], F32, name="ratio")
         for k in range(NPIECE):
             nc.scalar.activation(expo[:, pieces[k]], z[CORE, k][:], FUNC.Exp, bias=offsets_c[:, 0:1], scale=slopes_c[:, 0:1])
         for k in range(NPIECE // 2):
-            nc.scalar.activation(excess[:, pieces[k]], z[CORE, k][:], FUNC.Relu, bias=offsets_c[:, 1:2], scale=slopes_c[:, 1:2])
+            nc.scalar.activation(ratio[:, pieces[k]], z[CORE, k][:], FUNC.Identity, bias=offsets_c[:, 1:2], scale=slopes_c[:, 1:2])
         for k in range(NPIECE // 2, NPIECE):
-            nc.vector.tensor_scalar(excess[:, pieces[k]], z[CORE, k][:], slopes_c[:, 1:2], offsets_c[:, 1:2], ALU.mult, ALU.add)
-        nc.vector.tensor_scalar_max(excess[:, N // 2 : N], excess[:, N // 2 : N], 0.0)
+            nc.vector.tensor_scalar(ratio[:, pieces[k]], z[CORE, k][:], slopes_c[:, 1:2], offsets_c[:, 1:2], ALU.mult, ALU.add)
 
         measure(GATE)
         affine_g = held.tile([P, 2], F32, tag="gate_then_log", name="affine_g")
@@ -170,27 +168,18 @@ def tile_convlayer_kernel(tc, table, w_self, w_nbr, w_edge, edge, gamma1, beta1,
         for h in range(NPIECE // 2):
             nc.vector.tensor_scalar_min(capped[:, wide[h]], expo[:, wide[h]], exp_clamp[:])
 
-        gated_excess = held.tile([P, N], F32, name="gated_excess")
-        early_pairs = held.tile([P, N // 2], F32, name="early_pairs")
-        early = held.tile([P, S], F32, name="early")
         for h in range(NPIECE // 2):
-            nc.vector.scalar_tensor_tensor(
-                gated_excess[:, wide[h]], tanh_g[:, wide[h]], 1.0, excess[:, wide[h]], ALU.add, ALU.mult
-            )
+            nc.vector.tensor_scalar_max(ratio[:, wide[h]], ratio[:, wide[h]], 0.5)
+        factor = held.tile([P, N], F32, name="factor")
         for h in range(NPIECE // 2):
-            sum_over_bonds(early[:, wide_atoms[h]], gated_excess[:, wide[h]], early_pairs[:, wide_pairs[h]])
+            nc.vector.scalar_tensor_tensor(factor[:, wide[h]], tanh_g[:, wide[h]], 1.0, ratio[:, wide[h]], ALU.add, ALU.mult)
 
         log1p = held.tile([P, N], F32, tag="gate_then_log", name="log1p")
-        gated_log = held.tile([P, N], F32, name="gated_log")
-        late_pairs = held.tile([P, N // 2], F32, name="late_pairs")
-        late = held.tile([P, S], F32, name="late")
+        message = held.tile([P, N], F32, name="message")
+        pair_sums = held.tile([P, N // 2], F32, name="pair_sums")
         out_sb = held.tile([P, S], F32, name="out_sb")
         for h in range(NPIECE // 2):
             nc.scalar.activation(log1p[:, wide[h]], capped[:, wide[h]], FUNC.Ln, bias=one[:])
-            nc.vector.scalar_tensor_tensor(
-                gated_log[:, wide[h]], tanh_g[:, wide[h]], 1.0, log1p[:, wide[h]], ALU.add, ALU.mult
-            )
-            sum_over_bonds(late[:, wide_atoms[h]], gated_log[:, wide[h]], late_pairs[:, wide_pairs[h]])
-            done = wide_atoms[h]
-            nc.vector.scalar_tensor_tensor(out_sb[:, done], late[:, done], 0.5, early[:, done], ALU.mult, ALU.add)
-            nc.sync.dma_start(out[:, done], out_sb[:, done])
+            nc.vector.tensor_tensor(message[:, wide[h]], factor[:, wide[h]], log1p[:, wide[h]], ALU.mult)
+            sum_over_bonds(out_sb[:, wide_atoms[h]], message[:, wide[h]], pair_sums[:, wide_pairs[h]])
+            nc.sync.dma_start(out[:, wide_atoms[h]], out_sb[:, wide_atoms[h]])

@@ -59,8 +59,8 @@ def tile_convlayer_kernel(tc, table, w_self, w_nbr, w_edge, edge, gamma1, beta1,
         gamma_sb = held.tile([P, 2], F32, name="gamma_sb")
         beta_sb = held.tile([P, 2], F32, name="beta_sb")
         with nc.allow_non_contiguous_dma(reason="one float to a partition, 256 in all"):
-            nc.scalar.dma_start(gamma_sb[:], gamma1.rearrange("(b p) o -> p (b o)", p=P))
-            nc.scalar.dma_start(beta_sb[:], beta1.rearrange("(b p) o -> p (b o)", p=P))
+            nc.sync.dma_start(gamma_sb[:], gamma1.rearrange("(b p) o -> p (b o)", p=P))
+            nc.sync.dma_start(beta_sb[:], beta1.rearrange("(b p) o -> p (b o)", p=P))
 
         exp_clamp = held.tile([P, 1], F32, name="exp_clamp")
         nc.scalar.activation(exp_clamp[:], one[:], FUNC.Exp, scale=CLAMP)
@@ -69,7 +69,7 @@ def tile_convlayer_kernel(tc, table, w_self, w_nbr, w_edge, edge, gamma1, beta1,
         nc.scalar.activation(signed_gamma_c[:], signs_and_scales[:], FUNC.Identity, scale=gamma_sb[:, CORE : CORE + 1])
         small_beta_c = held.tile([P, 1], F32, name="small_beta_c")
         nc.scalar.mul(small_beta_c[:], beta_sb[:, CORE : CORE + 1], SMALL)
-        factors_g = held.tile([P, 2], F32, name="factors_g")
+        factors_g = held.tile([P, 2], F32, tag="factors_then_ratio", name="factors_g")
         nc.scalar.mul(factors_g[:, 0:1], gamma_sb[:, GATE : GATE + 1], 0.5)
         neg_half_gamma_g = held.tile([P, 1], F32, name="neg_half_gamma_g")
         nc.scalar.mul(neg_half_gamma_g[:], gamma_sb[:, GATE : GATE + 1], -0.5)
@@ -138,13 +138,11 @@ def tile_convlayer_kernel(tc, table, w_self, w_nbr, w_edge, edge, gamma1, beta1,
                 scale=slopes_c[:, 2 + line : 3 + line],
             )
         expo = held.tile([P, N], F32, name="expo")
-        ratio = held.tile([P, N], F32, name="ratio")
+        ratio = [held.tile([P, N // 2], F32, name="ratio0")]
         for k in range(NPIECE):
             nc.scalar.activation(expo[:, pieces[k]], z[CORE, k][:], FUNC.Exp, bias=offsets_c[:, 0:1], scale=slopes_c[:, 0:1])
         for k in range(NPIECE // 2):
-            nc.scalar.activation(ratio[:, pieces[k]], z[CORE, k][:], FUNC.Identity, bias=offsets_c[:, 1:2], scale=slopes_c[:, 1:2])
-        for k in range(NPIECE // 2, NPIECE):
-            nc.vector.tensor_scalar(ratio[:, pieces[k]], z[CORE, k][:], slopes_c[:, 1:2], offsets_c[:, 1:2], ALU.mult, ALU.add)
+            nc.scalar.activation(ratio[0][:, pieces[k]], z[CORE, k][:], FUNC.Identity, bias=offsets_c[:, 1:2], scale=slopes_c[:, 1:2])
 
         measure(GATE)
         affine_g = held.tile([P, 2], F32, tag="gate_then_log", name="affine_g")
@@ -168,11 +166,16 @@ def tile_convlayer_kernel(tc, table, w_self, w_nbr, w_edge, edge, gamma1, beta1,
         for h in range(NPIECE // 2):
             nc.vector.tensor_scalar_min(capped[:, wide[h]], expo[:, wide[h]], exp_clamp[:])
 
-        for h in range(NPIECE // 2):
-            nc.vector.tensor_scalar_max(ratio[:, wide[h]], ratio[:, wide[h]], 0.5)
+        ratio.append(held.tile([P, N // 2], F32, tag="factors_then_ratio", name="ratio1"))
+        for k in range(NPIECE // 2, NPIECE):
+            nc.vector.tensor_scalar(
+                ratio[1][:, pieces[k - NPIECE // 2]], z[CORE, k][:], slopes_c[:, 1:2], offsets_c[:, 1:2], ALU.mult, ALU.add
+            )
         factor = held.tile([P, N], F32, name="factor")
         for h in range(NPIECE // 2):
-            nc.vector.scalar_tensor_tensor(factor[:, wide[h]], tanh_g[:, wide[h]], 1.0, ratio[:, wide[h]], ALU.add, ALU.mult)
+            nc.vector.tensor_scalar_max(ratio[h][:], ratio[h][:], 0.5)
+        for h in range(NPIECE // 2):
+            nc.vector.scalar_tensor_tensor(factor[:, wide[h]], tanh_g[:, wide[h]], 1.0, ratio[h][:], ALU.add, ALU.mult)
 
         log1p = held.tile([P, N], F32, tag="gate_then_log", name="log1p")
         message = held.tile([P, N], F32, name="message")

@@ -10,7 +10,7 @@ ATOMS = PIECE // T
 GATE, CORE = 0, 1
 CLAMP = 30.0
 SMALL = 1 / (2 * CLAMP)
-WARM_UP = 4
+WARM_UP = 3
 FLOPS = 2 * F * (N * D + S * D + N * E)
 
 BF16, F32, U16 = mybir.dt.bfloat16, mybir.dt.float32, mybir.dt.uint16

import concourse.mybir as mybir
from concourse.masks import make_identity

P = 128
S, D, E, F, T, N = 256, 128, 128, 256, 4, 1024
EPS = 1e-5
PIECE = S
NPIECE = N // PIECE
ATOMS = PIECE // T
GATE, CORE = 0, 1
CLAMP = 30.0
SMALL = 1 / (2 * CLAMP)
WARM_UP = 3
FLOPS = 2 * F * (N * D + S * D + N * E)

BF16, F32, U16 = mybir.dt.bfloat16, mybir.dt.float32, mybir.dt.uint16
ALU = mybir.AluOpType
FUNC = mybir.ActivationFunctionType


def tile_convlayer_kernel(tc, table, w_self, w_nbr, w_edge, edge, gamma1, beta1, offs, out):
    nc = tc.nc
    pieces = [slice(k * PIECE, (k + 1) * PIECE) for k in range(NPIECE)]
    atoms = [slice(k * ATOMS, (k + 1) * ATOMS) for k in range(NPIECE)]
    features = [slice(blk * P, (blk + 1) * P) for blk in range(2)]
    with (
        tc.tile_pool(name="held", bufs=1) as held,
        tc.psum_pool(name="banks", bufs=8) as banks,
    ):
        zeros = held.tile([P, 32], BF16, name="zeros")
        nc.gpsimd.memset(zeros[:], 0.0)
        unread = banks.tile([32, 16, 32], F32, tag="bank", name="unread")
        for turn in range(WARM_UP):
            nc.tensor.matmul(unread[:], zeros[:], zeros[:].unsqueeze(1).to_broadcast([P, 16, 32]), start=True, stop=True)

        ident = held.tile([P, P], BF16, name="ident")
        make_identity(nc, ident[:])
        neg_half = held.tile([P, 1], F32, name="neg_half")
        nc.gpsimd.memset(neg_half[:], -0.5)
        one = held.tile([P, 1], F32, name="one")
        nc.vector.memset(one[:], 1.0)
        signs_and_scales = held.tile([P, 4], F32, name="signs_and_scales")
        for i, weight in enumerate((1.0, SMALL, -1.0, -SMALL)):
            nc.vector.memset(signs_and_scales[:, i : i + 1], weight)

        rows = held.tile([P, S // P, D], BF16, name="rows")
        nc.sync.dma_start(rows[:], table.rearrange("(b p) d -> p b d", p=P))
        w_edge_sb = held.tile([P, F], BF16, name="w_edge_sb")
        nc.sync.dma_start(w_edge_sb[:], w_edge)
        edge_sb = [held.tile([P, N // 2], BF16, name=f"edge_sb{h}") for h in range(2)]
        for h in range(2):
            nc.sync.dma_start(edge_sb[h][:], edge[:, h * (N // 2) : (h + 1) * (N // 2)])
        w_self_sb = held.tile([P, F], BF16, name="w_self_sb")
        nc.sync.dma_start(w_self_sb[:], w_self)
        offsets = held.tile([P, N // 16], U16, name="offsets")
        nc.sync.dma_start(offsets[:], offs)
        w_nbr_sb = held.tile([P, F], BF16, name="w_nbr_sb")
        nc.sync.dma_start(w_nbr_sb[:], w_nbr)
        gamma_sb = held.tile([P, 2], F32, name="gamma_sb")
        beta_sb = held.tile([P, 2], F32, name="beta_sb")
        with nc.allow_non_contiguous_dma(reason="one float to a partition, 256 in all"):
            nc.sync.dma_start(gamma_sb[:], gamma1.rearrange("(b p) o -> p (b o)", p=P))
            nc.sync.dma_start(beta_sb[:], beta1.rearrange("(b p) o -> p (b o)", p=P))

        exp_clamp = held.tile([P, 1], F32, name="exp_clamp")
        nc.scalar.activation(exp_clamp[:], one[:], FUNC.Exp, scale=CLAMP)

        signed_gamma_c = held.tile([P, 4], F32, name="signed_gamma_c")
        nc.scalar.activation(signed_gamma_c[:], signs_and_scales[:], FUNC.Identity, scale=gamma_sb[:, CORE : CORE + 1])
        small_beta_c = held.tile([P, 1], F32, name="small_beta_c")
        nc.scalar.mul(small_beta_c[:], beta_sb[:, CORE : CORE + 1], SMALL)
        factors_g = held.tile([P, 2], F32, tag="factors_then_ratio", name="factors_g")
        nc.scalar.mul(factors_g[:, 0:1], gamma_sb[:, GATE : GATE + 1], 0.5)
        neg_half_gamma_g = held.tile([P, 1], F32, name="neg_half_gamma_g")
        nc.scalar.mul(neg_half_gamma_g[:], gamma_sb[:, GATE : GATE + 1], -0.5)
        addends_g = held.tile([P, 2], F32, name="addends_g")
        nc.vector.memset(addends_g[:, 0:1], 0.0)
        nc.scalar.mul(addends_g[:, 1:2], beta_sb[:, GATE : GATE + 1], 0.5)

        flipped = banks.tile([P, S], BF16, tag="bank", name="flipped")
        for b in range(S // P):
            nc.tensor.transpose(flipped[:, b * P : (b + 1) * P], rows[:, b, :], ident[:])
        tab_t = held.tile([P, S], BF16, name="tab_t")
        nc.vector.tensor_copy(tab_t[:], flipped[:])

        z = {}
        for blk in (CORE, GATE):
            for k in range(NPIECE):
                z[blk, k] = banks.tile([P, PIECE], F32, tag="bank", name=f"z{blk}_{k}")

        def edge_product(blk, k, start, stop):
            nc.tensor.matmul(z[blk, k][:], w_edge_sb[:, features[blk]], edge_sb[k // 2][:, pieces[k % 2]], start=start, stop=stop)

        def own_product(blk, k, start, stop):
            own = tab_t[:, atoms[k]].unsqueeze(2).to_broadcast([P, ATOMS, T])
            nc.tensor.matmul(
                z[blk, k][:].rearrange("p (i t) -> p i t", t=T), w_self_sb[:, features[blk]], own, start=start, stop=stop
            )

        def neighbour_product(blk, k, start, stop):
            neighbours = tab_t[:].indirect(offsets[:, k * (PIECE // 16) : (k + 1) * (PIECE // 16)])
            nc.tensor.matmul(z[blk, k][:], w_nbr_sb[:, features[blk]], neighbours, start=start, stop=stop)

        for k in range(NPIECE):
            edge_product(CORE, k, start=True, stop=False)
        for k in range(NPIECE):
            own_product(CORE, k, start=False, stop=False)
        for k in range(NPIECE):
            neighbour_product(CORE, k, start=False, stop=True)
        for k in range(NPIECE):
            neighbour_product(GATE, k, start=True, stop=False)
        for k in range(NPIECE):
            edge_product(GATE, k, start=False, stop=False)
            own_product(GATE, k, start=False, stop=True)

        stats = held.tile([P, 2, NPIECE, 6], F32, name="stats")
        moments = held.tile([P, 2, 2], F32, name="moments")
        rstd = held.tile([P, 2], F32, tag="rstd_then_capped", name="rstd")

        def measure(blk):
            for k in range(NPIECE):
                nc.vector.bn_stats(stats[:, blk, k, :], z[blk, k][:])
                if k == 0:
                    nc.vector.tensor_scalar_add(stats[:, blk, 0, 2:3], stats[:, blk, 0, 2:3], N * EPS)
            nc.vector.bn_aggr(moments[:, blk, :], stats[:, blk, :, :])
            nc.gpsimd.tensor_tensor(rstd[:, blk : blk + 1], moments[:, blk, 1:2], neg_half[:], ALU.pow)

        measure(CORE)
        slopes_c = held.tile([P, 4], F32, name="slopes_c")
        nc.scalar.activation(slopes_c[:], signed_gamma_c[:], FUNC.Identity, scale=rstd[:, CORE : CORE + 1])
        offsets_c = held.tile([P, 2], F32, name="offsets_c")
        for line, addend in enumerate((beta_sb[:, CORE : CORE + 1], small_beta_c[:])):
            nc.scalar.activation(
                offsets_c[:, line : line + 1],
                moments[:, CORE, 0:1],
                FUNC.Identity,
                bias=addend,
                scale=slopes_c[:, 2 + line : 3 + line],
            )
        expo = held.tile([P, N], F32, name="expo")
        ratio = [held.tile([P, N // 2], F32, name="ratio0")]
        for k in range(NPIECE):
            nc.scalar.activation(expo[:, pieces[k]], z[CORE, k][:], FUNC.Exp, bias=offsets_c[:, 0:1], scale=slopes_c[:, 0:1])
        for k in range(NPIECE // 2):
            nc.scalar.activation(ratio[0][:, pieces[k]], z[CORE, k][:], FUNC.Identity, bias=offsets_c[:, 1:2], scale=slopes_c[:, 1:2])

        measure(GATE)
        affine_g = held.tile([P, 2], F32, tag="gate_then_log", name="affine_g")
        nc.vector.tensor_scalar_mul(factors_g[:, 1:2], neg_half_gamma_g[:], moments[:, GATE, 0:1])
        nc.vector.scalar_tensor_tensor(affine_g[:], factors_g[:], rstd[:, GATE : GATE + 1], addends_g[:], ALU.mult, ALU.add)
        tanh_g = held.tile([P, N], F32, name="tanh_g")
        for k in range(NPIECE):
            nc.scalar.activation(tanh_g[:, pieces[k]], z[GATE, k][:], FUNC.Tanh, bias=affine_g[:, 1:2], scale=affine_g[:, 0:1])

        wide = [slice(h * 2 * PIECE, (h + 1) * 2 * PIECE) for h in range(NPIECE // 2)]
        wide_atoms = [slice(h * 2 * ATOMS, (h + 1) * 2 * ATOMS) for h in range(NPIECE // 2)]
        wide_pairs = [slice(h * PIECE, (h + 1) * PIECE) for h in range(NPIECE // 2)]

        def sum_over_bonds(sums, terms, pairs):
            by_bond = terms.rearrange("p (i t) -> p i t", t=T)
            by_pair = pairs.rearrange("p (i u) -> p i u", u=2)
            nc.vector.tensor_tensor(by_pair, by_bond[:, :, 0:2], by_bond[:, :, 2:4], ALU.add)
            nc.vector.tensor_tensor(sums, by_pair[:, :, 0], by_pair[:, :, 1], ALU.add)

        capped = held.tile([P, N], F32, tag="rstd_then_capped", name="capped")
        for h in range(NPIECE // 2):
            nc.vector.tensor_scalar_min(capped[:, wide[h]], expo[:, wide[h]], exp_clamp[:])

        ratio.append(held.tile([P, N // 2], F32, tag="factors_then_ratio", name="ratio1"))
        for k in range(NPIECE // 2, NPIECE):
            nc.vector.tensor_scalar(
                ratio[1][:, pieces[k - NPIECE // 2]], z[CORE, k][:], slopes_c[:, 1:2], offsets_c[:, 1:2], ALU.mult, ALU.add
            )
        factor = held.tile([P, N], F32, name="factor")
        for h in range(NPIECE // 2):
            nc.vector.tensor_scalar_max(ratio[h][:], ratio[h][:], 0.5)
        for h in range(NPIECE // 2):
            nc.vector.scalar_tensor_tensor(factor[:, wide[h]], tanh_g[:, wide[h]], 1.0, ratio[h][:], ALU.add, ALU.mult)

        log1p = held.tile([P, N], F32, tag="gate_then_log", name="log1p")
        message = held.tile([P, N], F32, name="message")
        pair_sums = held.tile([P, N // 2], F32, name="pair_sums")
        out_sb = held.tile([P, S], F32, name="out_sb")
        for h in range(NPIECE // 2):
            nc.scalar.activation(log1p[:, wide[h]], capped[:, wide[h]], FUNC.Ln, bias=one[:])
            nc.vector.tensor_tensor(message[:, wide[h]], factor[:, wide[h]], log1p[:, wide[h]], ALU.mult)
            sum_over_bonds(out_sb[:, wide_atoms[h]], message[:, wide[h]], pair_sums[:, wide_pairs[h]])
            nc.sync.dma_start(out[:, wide_atoms[h]], out_sb[:, wide_atoms[h]])
